import numpy as np
import ml_dtypes


def mxq(x, axis, fmt="e4m3"):
    dtype, down = {"e4m3": (ml_dtypes.float8_e4m3fn, 7), "e5m2": (ml_dtypes.float8_e5m2, 14)}[fmt]
    v = np.moveaxis(np.asarray(x, np.float32).astype(ml_dtypes.bfloat16).astype(np.float64), axis, -1)
    blocks = v.reshape(v.shape[:-1] + (-1, 32))
    amax = np.abs(blocks).max(-1, keepdims=True)
    byte = np.maximum(np.where(amax > 0, np.frexp(amax)[1] - 1 + 127, 0) - down, 1)
    scale = np.exp2(byte - 127.0)
    codes = (blocks / scale).astype(np.float32).astype(dtype).astype(np.float64)
    return np.moveaxis((codes * scale).reshape(v.shape), -1, axis)


WIDE = False


def mx_kscale(k):
    if not WIDE:
        return np.ones(k)
    levels = np.array([10, -10, 5, -5, 0])
    a = np.random.permutation(np.resize(levels, k // 512 * 4)).reshape(k // 512, 4)
    idx = np.arange(k)
    return np.exp2(a[idx // 512, idx % 128 // 32])


BF16 = ml_dtypes.bfloat16


def bf(x):
    return np.asarray(x, np.float32).astype(BF16)


def f64(x):
    return np.asarray(x).astype(np.float64)


B, D, N, K = 4, 512, 4096, 128
EPS = 1e-06


def l2_normalize(v, axis):
    nrm = np.sqrt(np.sum(v * v, axis=axis, keepdims=True))
    return v / np.maximum(nrm, EPS)


def setup_inputs():
    r = np.sqrt(D)
    u = np.exp2(np.round(np.log2(mx_kscale(N)) / 2))
    c = np.exp2(np.round(np.log2(np.mean(u * u)) / 2))
    g = 1.8 * np.random.standard_normal((B, K, N)) + 2.3 * np.random.standard_normal((B, K, 1))
    e = np.exp(g - g.max(axis=1, keepdims=True))
    probs = e / e.sum(axis=1, keepdims=True)
    x = (10.0 * np.random.standard_normal((B, D, N)) + 6.0 * np.random.standard_normal((B, D, 1))) / r
    mu = 3.5 * np.random.standard_normal((1, D, K)) / r
    sigma = 1.0 + 9.0 / r * (np.random.random((1, D, K)) - 0.5)
    return {"probs": bf(probs * (u * u)), "x": bf(x * (c / u)), "mu": bf(mu), "sigma": bf(sigma)}


def reference(probs, x, mu, sigma):
    probs, x, mu, sigma = f64(probs), f64(x), f64(mu), f64(sigma)
    probs_norm = probs / (np.sum(probs, axis=2, keepdims=True) + EPS)
    pq = mxq(probs_norm, 2, "e4m3").transpose(0, 2, 1)
    x2 = x * x
    weighted_mu = mxq(x, 2, "e4m3") @ pq
    weighted_x2 = mxq(x2, 2, "e4m3") @ pq
    sigma_hat = np.sqrt(np.maximum(weighted_x2 - weighted_mu * weighted_mu, EPS))
    feat = np.concatenate([weighted_mu - mu, sigma_hat - sigma], axis=1)
    feat = l2_normalize(feat, 1)
    feat = feat.reshape(B, -1)
    return l2_normalize(feat, 1)

@@ -1,0 +1,275 @@
+from contextlib import ExitStack
+
+import concourse.mybir as mybir
+from concourse.masks import make_identity
+
+F32 = mybir.dt.float32
+BF16 = mybir.dt.bfloat16
+U32 = mybir.dt.uint32
+U8 = mybir.dt.uint8
+FP8X4 = mybir.dt.float8_e4m3fn_x4
+ACT = mybir.ActivationFunctionType
+ALU = mybir.AluOpType
+
+P = 128
+BATCHES, FEATURES, POINTS, CLUSTERS = 4, 512, 4096, 128
+EPS = 1e-6
+FLOPS = 2 * 2 * BATCHES * FEATURES * POINTS * CLUSTERS
+
+PASS_POINTS = 4 * P
+PASS_WORDS = PASS_POINTS // 2
+PASSES = POINTS // PASS_POINTS
+CHUNKS = FEATURES // P
+UNIT_PASSES = 2
+UNIT_POINTS = UNIT_PASSES * PASS_POINTS
+BATCH_UNITS = POINTS // UNIT_POINTS
+UNITS = BATCHES * BATCH_UNITS
+LOADS_AHEAD = 4
+MULTIPLY_LAG = 2
+
+
+def tile_wassvladlayer_pb_kernel(tc, probs, x, mu, sigma, out):
+    nc = tc.nc
+    with ExitStack() as pools:
+        consts = pools.enter_context(tc.tile_pool(name="consts", bufs=1))
+        x_pool = pools.enter_context(tc.tile_pool(name="x_pool", bufs=LOADS_AHEAD))
+        p_raw_pool = pools.enter_context(tc.tile_pool(name="p_raw_pool", bufs=2))
+        p_pool = pools.enter_context(tc.tile_pool(name="p_pool", bufs=1))
+        p_codes_pool = pools.enter_context(tc.tile_pool(name="p_codes_pool", bufs=2))
+        grouped_pool = pools.enter_context(tc.tile_pool(name="grouped_pool", bufs=3 * UNIT_PASSES))
+        codes_pool = pools.enter_context(tc.tile_pool(name="codes_pool", bufs=(MULTIPLY_LAG + 2) * UNIT_PASSES))
+        tail_pool = pools.enter_context(tc.tile_pool(name="tail_pool", bufs=1))
+        flip_psum = pools.enter_context(tc.psum_pool(name="flip_psum", bufs=4))
+        acc_psum = pools.enter_context(tc.psum_pool(name="acc_psum", bufs=2))
+
+        held = {}
+
+        ident = consts.tile([P, P], F32, name="ident")
+        make_identity(nc, ident)
+        ones = consts.tile([P, P], F32, name="ones")
+        nc.vector.memset(ones, 1.0)
+        one = consts.tile([P, 1], F32, name="one")
+        nc.vector.memset(one, 1.0)
+        root_of_one = consts.tile([P, 1], F32, name="root_of_one")
+        nc.scalar.activation(out=root_of_one, in_=one, func=ACT.Sqrt)
+
+        def load_probs(b):
+            raw = p_raw_pool.tile([P, POINTS], BF16, name="p_raw")
+            nc.sync.dma_start(out=raw, in_=probs[b])
+            held["p_raw", b] = raw
+
+        def load_x(u):
+            b, j = divmod(u, BATCH_UNITS)
+            raw = x_pool.tile([P, CHUNKS, UNIT_POINTS], BF16, name="x_raw")
+            rows = x[b].rearrange("(p c) n -> p c n", c=CHUNKS)
+            nc.sync.dma_start(out=raw, in_=rows[:, :, j * UNIT_POINTS : (j + 1) * UNIT_POINTS])
+            held["x_raw", u] = raw
+
+        def load_param(param, name):
+            raw = consts.tile([P, CHUNKS, CLUSTERS], BF16, name=name + "_raw")
+            nc.scalar.dma_start(out=raw, in_=param[0].rearrange("(p c) k -> p c k", c=CHUNKS))
+            return raw
+
+        def cluster_rows(raw, name):
+            wide = consts.tile([P, CHUNKS, CLUSTERS], F32, name=name + "_wide")
+            nc.vector.tensor_copy(out=wide, in_=raw)
+            back = flip_psum.tile([P, CHUNKS, P], F32, name="param_back", tag="flipped")
+            for c in range(CHUNKS):
+                nc.tensor.transpose(back[:, c, :], wide[:, c, :], ident)
+            rows = consts.tile([P, FEATURES], F32, name=name + "_rows")
+            nc.scalar.copy(out=rows, in_=back.rearrange("p c d -> p (c d)"))
+            return rows
+
+        def flip_bank(two_blocks, grouped_words):
+            flipped = flip_psum.tile([P, 2, 2, P], F32, name="flipped")
+            for i, words in enumerate(two_blocks):
+                for half in range(2):
+                    nc.tensor.transpose(flipped[:, i, half, :], words[:, half * P : (half + 1) * P], ident)
+            nc.scalar.copy(out=grouped_words, in_=flipped.rearrange("q i half row -> q i row half"))
+
+        def as_blocks(grouped):
+            return grouped.bitcast(F32).rearrange("q (blk row half) -> q blk row half", row=P, half=2)
+
+        def quantise(pool, grouped, name):
+            width = grouped.shape[1] // 4
+            codes = pool.tile([P, width], U32, name=name + "_codes", align_bytes=64)
+            scales = pool.tile([P, width], U8, name=name + "_scales", align_bytes=64)
+            nc.vector.quantize_mx(out=codes.bitcast(FP8X4), scales=scales, in_=grouped)
+            return codes, scales
+
+        def normalise_p(b):
+            raw = held["p_raw", b]
+            p_rows = p_pool.tile([P, POINTS], BF16, name="p_rows")
+            total = p_pool.tile([P, 1], F32, name="p_total")
+            nc.vector.tensor_scalar(
+                out=p_rows, in0=raw, scalar1=1.0, scalar2=None, op0=ALU.mult, op1=ALU.add, accum_out=total
+            )
+            padded = p_pool.tile([P, 1], F32, name="p_padded")
+            nc.vector.tensor_scalar_add(out=padded, in0=total, scalar1=EPS)
+            share = p_pool.tile([P, 1], F32, name="p_share")
+            nc.vector.reciprocal(out=share, in_=padded)
+            nc.vector.tensor_scalar_mul(out=p_rows, in0=raw, scalar1=share[:, 0:1])
+            held["p_rows", b] = p_rows
+            if b + 2 < BATCHES:
+                load_probs(b + 2)
+
+        def flip_p(b):
+            words = held["p_rows", b].bitcast(F32)
+            grouped = p_pool.tile([P, POINTS], BF16, name="p_grouped", align_bytes=64)
+            blocks = as_blocks(grouped)
+            for g in range(0, PASSES, 2):
+                two = [words[:, (g + i) * PASS_WORDS : (g + i + 1) * PASS_WORDS] for i in range(2)]
+                flip_bank(two, blocks[:, g : g + 2])
+            held["p_grouped", b] = grouped
+
+        def quantise_p(b):
+            held["p_mx", b] = quantise(p_codes_pool, held["p_grouped", b], "p")
+
+        p_stages = (normalise_p, flip_p, quantise_p)
+
+        def flip_x(u):
+            words = held["x_raw", u].bitcast(F32)
+            for g in range(UNIT_PASSES):
+                grouped = grouped_pool.tile([P, 4 * FEATURES], BF16, name="x_grouped", align_bytes=64)
+                blocks = as_blocks(grouped)
+                for c in range(0, CHUNKS, 2):
+                    two = [words[:, c + i, g * PASS_WORDS : (g + 1) * PASS_WORDS] for i in range(2)]
+                    flip_bank(two, blocks[:, c : c + 2])
+                held["x_grouped", u, g] = grouped
+
+        def square_and_quantise_x(u):
+            for g in range(UNIT_PASSES):
+                grouped = held["x_grouped", u, g]
+                squares = grouped_pool.tile([P, 4 * FEATURES], BF16, name="sq_grouped", align_bytes=64)
+                if g == 0:
+                    nc.vector.tensor_tensor(out=squares, in0=grouped, in1=grouped, op=ALU.mult)
+                else:
+                    nc.scalar.activation(out=squares, in_=grouped, func=ACT.Square)
+                held["sq_grouped", u, g] = squares
+            for what in ("x", "sq"):
+                for g in range(UNIT_PASSES):
+                    held[what + "_mx", u, g] = quantise(codes_pool, held[what + "_grouped", u, g], what)
+
+        def multiply(u):
+            b, j = divmod(u, BATCH_UNITS)
+            if j == 0:
+                held["m1", b] = acc_psum.tile([P, FEATURES], F32, name="m1")
+                held["m2", b] = acc_psum.tile([P, FEATURES], F32, name="m2")
+            p_codes, p_scales = held["p_mx", b]
+            for g in range(UNIT_PASSES):
+                whole = j * UNIT_PASSES + g
+                p_cols = slice(whole * CLUSTERS, (whole + 1) * CLUSTERS)
+                for acc, operand in (("m1", "x_mx"), ("m2", "sq_mx")):
+                    codes, scales = held[operand, u, g]
+                    nc.tensor.matmul_mx(
+                        out=held[acc, b],
+                        lhsT=p_codes[:, p_cols].bitcast(FP8X4),
+                        lhsT_scale=p_scales[:, p_cols],
+                        rhs=codes.bitcast(FP8X4),
+                        rhs_scale=scales,
+                        start=(whole == 0),
+                        stop=(whole == PASSES - 1),
+                    )
+
+        def variance(b):
+            m1_squared = tail_pool.tile([P, FEATURES], F32, name="m1_squared")
+            nc.scalar.activation(out=m1_squared, in_=held["m1", b], func=ACT.Square)
+            mean_part = tail_pool.tile([P, FEATURES], F32, name="mean_part")
+            nc.vector.tensor_tensor(out=mean_part, in0=held["m1", b], in1=mu_rows, op=ALU.subtract)
+            spread = tail_pool.tile([P, FEATURES], F32, name="spread")
+            nc.vector.tensor_tensor(out=spread, in0=held["m2", b], in1=m1_squared, op=ALU.subtract)
+            nc.vector.tensor_scalar_max(out=spread, in0=spread, scalar1=EPS)
+            held["spread", b] = spread
+            held["feat", b, 0] = mean_part
+
+        def deviation(b):
+            sigma_hat = tail_pool.tile([P, FEATURES], F32, name="sigma_hat")
+            nc.scalar.activation(out=sigma_hat, in_=held["spread", b], func=ACT.Sqrt)
+            unread = tail_pool.tile([P, FEATURES], F32, name="unread_0")
+            energy = tail_pool.tile([P, 1], F32, name="energy_0")
+            nc.scalar.activation(out=unread, in_=held["feat", b, 0], func=ACT.Square, accum_out=energy)
+            deviation_part = tail_pool.tile([P, FEATURES], F32, name="deviation_part")
+            nc.vector.tensor_tensor(out=deviation_part, in0=sigma_hat, in1=sigma_rows, op=ALU.subtract)
+            held["energy", b, 0] = energy
+            held["feat", b, 1] = deviation_part
+
+        def cluster_norm(b):
+            unread = tail_pool.tile([P, FEATURES], F32, name="unread_1")
+            energy = tail_pool.tile([P, 1], F32, name="energy_1")
+            nc.scalar.activation(out=unread, in_=held["feat", b, 1], func=ACT.Square, accum_out=energy)
+            norm = tail_pool.tile([P, 1], F32, name="norm")
+            nc.scalar.activation(out=norm, in_=energy, func=ACT.Sqrt, bias=held["energy", b, 0][:, 0:1])
+            floored = tail_pool.tile([P, 1], F32, name="floored")
+            nc.vector.tensor_scalar_max(out=floored, in0=norm, scalar1=EPS)
+            inverse = tail_pool.tile([P, 1], F32, name="inverse")
+            nc.vector.reciprocal(out=inverse, in_=floored)
+            partly = tail_pool.tile([P, 1], F32, name="partly")
+            nc.vector.tensor_scalar(
+                out=partly,
+                in0=energy,
+                scalar1=held["energy", b, 0][:, 0:1],
+                scalar2=inverse[:, 0:1],
+                op0=ALU.add,
+                op1=ALU.mult,
+            )
+            left = tail_pool.tile([P, 1], F32, name="left")
+            nc.vector.tensor_tensor(out=left, in0=partly, in1=inverse, op=ALU.mult)
+            held["left", b] = left
+            for h in range(2):
+                scaled = tail_pool.tile([P, FEATURES], F32, name="scaled_%d" % h)
+                nc.vector.tensor_scalar_mul(out=scaled, in0=held["feat", b, h], scalar1=inverse[:, 0:1])
+                held["scaled", b, h] = scaled
+
+        def whole_norm_and_store(b):
+            whole = flip_psum.tile([P, 1], F32, name="whole", tag="flipped")
+            nc.tensor.matmul(out=whole, lhsT=ones, rhs=held["left", b], start=True, stop=True)
+            norm = tail_pool.tile([P, 1], F32, name="whole_norm")
+            nc.scalar.activation(out=norm, in_=whole, func=ACT.Sqrt)
+            floored = tail_pool.tile([P, 1], F32, name="whole_floored")
+            nc.vector.tensor_scalar_max(out=floored, in0=norm, scalar1=EPS)
+            inverse = tail_pool.tile([P, 1], F32, name="whole_inverse")
+            nc.vector.reciprocal(out=inverse, in_=floored)
+            rows = out[b].rearrange("(h p ck) -> h p ck", h=2, p=P)
+            for h in range(2):
+                back = flip_psum.tile([P, CHUNKS, P], F32, name="back", tag="flipped")
+                for c in range(CHUNKS):
+                    nc.tensor.transpose(back[:, c, :], held["scaled", b, h][:, c * P : (c + 1) * P], ident)
+                result = tail_pool.tile([P, FEATURES], F32, name="result_%d" % h)
+                nc.vector.tensor_scalar_mul(
+                    out=result, in0=back.rearrange("p c k -> p (c k)"), scalar1=inverse[:, 0:1]
+                )
+                nc.sync.dma_start(out=rows[h], in_=result)
+
+        tail_stages = (variance, deviation, cluster_norm, whole_norm_and_store)
+
+        pools.enter_context(tc.manual_schedule())
+        mu_raw = load_param(mu, "mu")
+        sigma_raw = load_param(sigma, "sigma")
+        load_x(0)
+        load_probs(0)
+        load_x(1)
+        load_probs(1)
+        load_x(2)
+        load_x(3)
+        mu_rows = cluster_rows(mu_raw, "mu")
+        sigma_rows = cluster_rows(sigma_raw, "sigma")
+
+        for step in range(UNITS + MULTIPLY_LAG + len(tail_stages)):
+            if step < UNITS:
+                flip_x(step)
+                if step + LOADS_AHEAD < UNITS:
+                    load_x(step + LOADS_AHEAD)
+            for b in reversed(range(BATCHES)):
+                first = b * BATCH_UNITS
+                last_multiply = first + BATCH_UNITS - 1 + MULTIPLY_LAG
+                for i, stage in enumerate(tail_stages):
+                    if step == last_multiply + 1 + i:
+                        stage(b)
+            for b in range(BATCHES):
+                for i, stage in enumerate(p_stages):
+                    if step == max(b * BATCH_UNITS - 2, 0) + i:
+                        stage(b)
+            if MULTIPLY_LAG <= step < UNITS + MULTIPLY_LAG:
+                multiply(step - MULTIPLY_LAG)
+            if step < UNITS:
+                square_and_quantise_x(step)

@@ -22,10 +22,14 @@ PASSES = POINTS // PASS_POINTS
 CHUNKS = FEATURES // P
 UNIT_PASSES = 2
 UNIT_POINTS = UNIT_PASSES * PASS_POINTS
+UNIT_VALUES = CHUNKS * UNIT_POINTS
 BATCH_UNITS = POINTS // UNIT_POINTS
 UNITS = BATCHES * BATCH_UNITS
 LOADS_AHEAD = 4
 MULTIPLY_LAG = 2
+VECTOR_SQUARES = UNIT_VALUES * 5 // 8
+P_STAGE_LEADS = (4, 2, 1)
+TAIL_STAGE_GAP = 2
 
 
 def tile_wassvladlayer_pb_kernel(tc, probs, x, mu, sigma, out):
@@ -36,9 +40,9 @@ def tile_wassvladlayer_pb_kernel(tc, probs, x, mu, sigma, out):
         p_raw_pool = pools.enter_context(tc.tile_pool(name="p_raw_pool", bufs=2))
         p_pool = pools.enter_context(tc.tile_pool(name="p_pool", bufs=1))
         p_codes_pool = pools.enter_context(tc.tile_pool(name="p_codes_pool", bufs=2))
-        grouped_pool = pools.enter_context(tc.tile_pool(name="grouped_pool", bufs=3 * UNIT_PASSES))
-        codes_pool = pools.enter_context(tc.tile_pool(name="codes_pool", bufs=(MULTIPLY_LAG + 2) * UNIT_PASSES))
-        tail_pool = pools.enter_context(tc.tile_pool(name="tail_pool", bufs=1))
+        grouped_pool = pools.enter_context(tc.tile_pool(name="grouped_pool", bufs=3))
+        codes_pool = pools.enter_context(tc.tile_pool(name="codes_pool", bufs=MULTIPLY_LAG + 2))
+        tail_pool = pools.enter_context(tc.tile_pool(name="tail_pool", bufs=2))
         flip_psum = pools.enter_context(tc.psum_pool(name="flip_psum", bufs=4))
         acc_psum = pools.enter_context(tc.psum_pool(name="acc_psum", bufs=2))
 
@@ -46,8 +50,6 @@ def tile_wassvladlayer_pb_kernel(tc, probs, x, mu, sigma, out):
 
         ident = consts.tile([P, P], F32, name="ident")
         make_identity(nc, ident)
-        ones = consts.tile([P, P], F32, name="ones")
-        nc.vector.memset(ones, 1.0)
         one = consts.tile([P, 1], F32, name="one")
         nc.vector.memset(one, 1.0)
         root_of_one = consts.tile([P, 1], F32, name="root_of_one")
@@ -80,20 +82,21 @@ def tile_wassvladlayer_pb_kernel(tc, probs, x, mu, sigma, out):
             nc.scalar.copy(out=rows, in_=back.rearrange("p c d -> p (c d)"))
             return rows
 
-        def flip_bank(two_blocks, grouped_words):
-            flipped = flip_psum.tile([P, 2, 2, P], F32, name="flipped")
-            for i, words in enumerate(two_blocks):
-                for half in range(2):
-                    nc.tensor.transpose(flipped[:, i, half, :], words[:, half * P : (half + 1) * P], ident)
-            nc.scalar.copy(out=grouped_words, in_=flipped.rearrange("q i half row -> q i row half"))
-
-        def as_blocks(grouped):
-            return grouped.bitcast(F32).rearrange("q (blk row half) -> q blk row half", row=P, half=2)
+        def points_onto_partitions(blocks_of_words, grouped):
+            grouped_words = grouped.bitcast(F32).rearrange("q (blk row half) -> q blk row half", row=P, half=2)
+            for first in range(0, len(blocks_of_words), 2):
+                flipped = flip_psum.tile([P, 2, 2, P], F32, name="flipped")
+                for i in range(2):
+                    words = blocks_of_words[first + i]
+                    for half in range(2):
+                        nc.tensor.transpose(flipped[:, i, half, :], words[:, half * P : (half + 1) * P], ident)
+                nc.scalar.copy(
+                    out=grouped_words[:, first : first + 2], in_=flipped.rearrange("q i half row -> q i row half")
+                )
 
         def quantise(pool, grouped, name):
-            width = grouped.shape[1] // 4
-            codes = pool.tile([P, width], U32, name=name + "_codes", align_bytes=64)
-            scales = pool.tile([P, width], U8, name=name + "_scales", align_bytes=64)
+            codes = pool.tile([P, UNIT_VALUES // 4], U32, name=name + "_codes", align_bytes=64)
+            scales = pool.tile([P, UNIT_VALUES // 4], U8, name=name + "_scales", align_bytes=64)
             nc.vector.quantize_mx(out=codes.bitcast(FP8X4), scales=scales, in_=grouped)
             return codes, scales
 
@@ -102,12 +105,10 @@ def tile_wassvladlayer_pb_kernel(tc, probs, x, mu, sigma, out):
             p_rows = p_pool.tile([P, POINTS], BF16, name="p_rows")
             total = p_pool.tile([P, 1], F32, name="p_total")
             nc.vector.tensor_scalar(
-                out=p_rows, in0=raw, scalar1=1.0, scalar2=None, op0=ALU.mult, op1=ALU.add, accum_out=total
+                out=p_rows, in0=raw, scalar1=1.0, scalar2=EPS, op0=ALU.mult, op1=ALU.add, accum_out=total
             )
-            padded = p_pool.tile([P, 1], F32, name="p_padded")
-            nc.vector.tensor_scalar_add(out=padded, in0=total, scalar1=EPS)
             share = p_pool.tile([P, 1], F32, name="p_share")
-            nc.vector.reciprocal(out=share, in_=padded)
+            nc.vector.reciprocal(out=share, in_=total)
             nc.vector.tensor_scalar_mul(out=p_rows, in0=raw, scalar1=share[:, 0:1])
             held["p_rows", b] = p_rows
             if b + 2 < BATCHES:
@@ -115,11 +116,8 @@ def tile_wassvladlayer_pb_kernel(tc, probs, x, mu, sigma, out):
 
         def flip_p(b):
             words = held["p_rows", b].bitcast(F32)
-            grouped = p_pool.tile([P, POINTS], BF16, name="p_grouped", align_bytes=64)
-            blocks = as_blocks(grouped)
-            for g in range(0, PASSES, 2):
-                two = [words[:, (g + i) * PASS_WORDS : (g + i + 1) * PASS_WORDS] for i in range(2)]
-                flip_bank(two, blocks[:, g : g + 2])
+            grouped = p_pool.tile([P, UNIT_VALUES], BF16, name="p_grouped", align_bytes=64)
+            points_onto_partitions([words[:, g * PASS_WORDS : (g + 1) * PASS_WORDS] for g in range(PASSES)], grouped)
             held["p_grouped", b] = grouped
 
         def quantise_p(b):
@@ -129,26 +127,22 @@ def tile_wassvladlayer_pb_kernel(tc, probs, x, mu, sigma, out):
 
         def flip_x(u):
             words = held["x_raw", u].bitcast(F32)
-            for g in range(UNIT_PASSES):
-                grouped = grouped_pool.tile([P, 4 * FEATURES], BF16, name="x_grouped", align_bytes=64)
-                blocks = as_blocks(grouped)
-                for c in range(0, CHUNKS, 2):
-                    two = [words[:, c + i, g * PASS_WORDS : (g + 1) * PASS_WORDS] for i in range(2)]
-                    flip_bank(two, blocks[:, c : c + 2])
-                held["x_grouped", u, g] = grouped
+            grouped = grouped_pool.tile([P, UNIT_VALUES], BF16, name="x_grouped", align_bytes=64)
+            points_onto_partitions(
+                [words[:, c, g * PASS_WORDS : (g + 1) * PASS_WORDS] for g in range(UNIT_PASSES) for c in range(CHUNKS)],
+                grouped,
+            )
+            held["x_grouped", u] = grouped
 
         def square_and_quantise_x(u):
-            for g in range(UNIT_PASSES):
-                grouped = held["x_grouped", u, g]
-                squares = grouped_pool.tile([P, 4 * FEATURES], BF16, name="sq_grouped", align_bytes=64)
-                if g == 0:
-                    nc.vector.tensor_tensor(out=squares, in0=grouped, in1=grouped, op=ALU.mult)
-                else:
-                    nc.scalar.activation(out=squares, in_=grouped, func=ACT.Square)
-                held["sq_grouped", u, g] = squares
-            for what in ("x", "sq"):
-                for g in range(UNIT_PASSES):
-                    held[what + "_mx", u, g] = quantise(codes_pool, held[what + "_grouped", u, g], what)
+            grouped = held["x_grouped", u]
+            squares = grouped_pool.tile([P, UNIT_VALUES], BF16, name="sq_grouped", align_bytes=64)
+            mine = slice(0, VECTOR_SQUARES)
+            rest = slice(VECTOR_SQUARES, UNIT_VALUES)
+            nc.vector.tensor_tensor(out=squares[:, mine], in0=grouped[:, mine], in1=grouped[:, mine], op=ALU.mult)
+            nc.scalar.activation(out=squares[:, rest], in_=grouped[:, rest], func=ACT.Square)
+            held["x_mx", u] = quantise(codes_pool, grouped, "x")
+            held["sq_mx", u] = quantise(codes_pool, squares, "sq")
 
         def multiply(u):
             b, j = divmod(u, BATCH_UNITS)
@@ -156,17 +150,18 @@ def tile_wassvladlayer_pb_kernel(tc, probs, x, mu, sigma, out):
                 held["m1", b] = acc_psum.tile([P, FEATURES], F32, name="m1")
                 held["m2", b] = acc_psum.tile([P, FEATURES], F32, name="m2")
             p_codes, p_scales = held["p_mx", b]
-            for g in range(UNIT_PASSES):
-                whole = j * UNIT_PASSES + g
-                p_cols = slice(whole * CLUSTERS, (whole + 1) * CLUSTERS)
-                for acc, operand in (("m1", "x_mx"), ("m2", "sq_mx")):
-                    codes, scales = held[operand, u, g]
+            for acc, operand in (("m1", "x_mx"), ("m2", "sq_mx")):
+                codes, scales = held[operand, u]
+                for g in range(UNIT_PASSES):
+                    whole = j * UNIT_PASSES + g
+                    p_cols = slice(whole * CLUSTERS, (whole + 1) * CLUSTERS)
+                    x_cols = slice(g * FEATURES, (g + 1) * FEATURES)
                     nc.tensor.matmul_mx(
                         out=held[acc, b],
                         lhsT=p_codes[:, p_cols].bitcast(FP8X4),
                         lhsT_scale=p_scales[:, p_cols],
-                        rhs=codes.bitcast(FP8X4),
-                        rhs_scale=scales,
+                        rhs=codes[:, x_cols].bitcast(FP8X4),
+                        rhs_scale=scales[:, x_cols],
                         start=(whole == 0),
                         stop=(whole == PASSES - 1),
                     )
@@ -174,102 +169,100 @@ def tile_wassvladlayer_pb_kernel(tc, probs, x, mu, sigma, out):
         def variance(b):
             m1_squared = tail_pool.tile([P, FEATURES], F32, name="m1_squared")
             nc.scalar.activation(out=m1_squared, in_=held["m1", b], func=ACT.Square)
-            mean_part = tail_pool.tile([P, FEATURES], F32, name="mean_part")
-            nc.vector.tensor_tensor(out=mean_part, in0=held["m1", b], in1=mu_rows, op=ALU.subtract)
+            feat = tail_pool.tile([P, 2 * FEATURES], F32, name="feat")
+            nc.vector.tensor_tensor(out=feat[:, :FEATURES], in0=held["m1", b], in1=mu_rows, op=ALU.subtract)
             spread = tail_pool.tile([P, FEATURES], F32, name="spread")
             nc.vector.tensor_tensor(out=spread, in0=held["m2", b], in1=m1_squared, op=ALU.subtract)
             nc.vector.tensor_scalar_max(out=spread, in0=spread, scalar1=EPS)
             held["spread", b] = spread
-            held["feat", b, 0] = mean_part
+            held["feat", b] = feat
 
         def deviation(b):
+            feat = held["feat", b]
             sigma_hat = tail_pool.tile([P, FEATURES], F32, name="sigma_hat")
             nc.scalar.activation(out=sigma_hat, in_=held["spread", b], func=ACT.Sqrt)
-            unread = tail_pool.tile([P, FEATURES], F32, name="unread_0")
-            energy = tail_pool.tile([P, 1], F32, name="energy_0")
-            nc.scalar.activation(out=unread, in_=held["feat", b, 0], func=ACT.Square, accum_out=energy)
-            deviation_part = tail_pool.tile([P, FEATURES], F32, name="deviation_part")
-            nc.vector.tensor_tensor(out=deviation_part, in0=sigma_hat, in1=sigma_rows, op=ALU.subtract)
-            held["energy", b, 0] = energy
-            held["feat", b, 1] = deviation_part
+            unread = tail_pool.tile([P, FEATURES], F32, name="unread_mean")
+            energy = tail_pool.tile([P, 1], F32, name="mean_energy")
+            nc.scalar.activation(out=unread, in_=feat[:, :FEATURES], func=ACT.Square, accum_out=energy)
+            nc.vector.tensor_tensor(out=feat[:, FEATURES:], in0=sigma_hat, in1=sigma_rows, op=ALU.subtract)
+            held["mean_energy", b] = energy
 
         def cluster_norm(b):
-            unread = tail_pool.tile([P, FEATURES], F32, name="unread_1")
-            energy = tail_pool.tile([P, 1], F32, name="energy_1")
-            nc.scalar.activation(out=unread, in_=held["feat", b, 1], func=ACT.Square, accum_out=energy)
+            unread = tail_pool.tile([P, FEATURES], F32, name="unread_deviation")
+            energy = tail_pool.tile([P, 1], F32, name="deviation_energy")
+            nc.scalar.activation(out=unread, in_=held["feat", b][:, FEATURES:], func=ACT.Square, accum_out=energy)
             norm = tail_pool.tile([P, 1], F32, name="norm")
-            nc.scalar.activation(out=norm, in_=energy, func=ACT.Sqrt, bias=held["energy", b, 0][:, 0:1])
+            nc.scalar.activation(out=norm, in_=energy, func=ACT.Sqrt, bias=held["mean_energy", b][:, 0:1])
             floored = tail_pool.tile([P, 1], F32, name="floored")
             nc.vector.tensor_scalar_max(out=floored, in0=norm, scalar1=EPS)
             inverse = tail_pool.tile([P, 1], F32, name="inverse")
             nc.vector.reciprocal(out=inverse, in_=floored)
-            partly = tail_pool.tile([P, 1], F32, name="partly")
-            nc.vector.tensor_scalar(
-                out=partly,
-                in0=energy,
-                scalar1=held["energy", b, 0][:, 0:1],
-                scalar2=inverse[:, 0:1],
-                op0=ALU.add,
-                op1=ALU.mult,
-            )
             left = tail_pool.tile([P, 1], F32, name="left")
-            nc.vector.tensor_tensor(out=left, in0=partly, in1=inverse, op=ALU.mult)
+            nc.vector.tensor_tensor(out=left, in0=norm, in1=inverse, op=ALU.mult)
+            held["inverse", b] = inverse
             held["left", b] = left
-            for h in range(2):
-                scaled = tail_pool.tile([P, FEATURES], F32, name="scaled_%d" % h)
-                nc.vector.tensor_scalar_mul(out=scaled, in0=held["feat", b, h], scalar1=inverse[:, 0:1])
-                held["scaled", b, h] = scaled
 
-        def whole_norm_and_store(b):
+        def whole_norm(b):
+            left = held["left", b]
             whole = flip_psum.tile([P, 1], F32, name="whole", tag="flipped")
-            nc.tensor.matmul(out=whole, lhsT=ones, rhs=held["left", b], start=True, stop=True)
+            nc.tensor.matmul(out=whole, lhsT=left[:, 0:1].to_broadcast([P, P]), rhs=left, start=True, stop=True)
             norm = tail_pool.tile([P, 1], F32, name="whole_norm")
             nc.scalar.activation(out=norm, in_=whole, func=ACT.Sqrt)
             floored = tail_pool.tile([P, 1], F32, name="whole_floored")
             nc.vector.tensor_scalar_max(out=floored, in0=norm, scalar1=EPS)
             inverse = tail_pool.tile([P, 1], F32, name="whole_inverse")
             nc.vector.reciprocal(out=inverse, in_=floored)
+            scaled = tail_pool.tile([P, 2 * FEATURES], F32, name="scaled")
+            nc.vector.tensor_scalar(
+                out=scaled,
+                in0=held["feat", b],
+                scalar1=held["inverse", b][:, 0:1],
+                scalar2=inverse[:, 0:1],
+                op0=ALU.mult,
+                op1=ALU.mult,
+            )
+            held["scaled", b] = scaled
+
+        def store(b):
             rows = out[b].rearrange("(h p ck) -> h p ck", h=2, p=P)
             for h in range(2):
                 back = flip_psum.tile([P, CHUNKS, P], F32, name="back", tag="flipped")
                 for c in range(CHUNKS):
-                    nc.tensor.transpose(back[:, c, :], held["scaled", b, h][:, c * P : (c + 1) * P], ident)
+                    first = (h * CHUNKS + c) * P
+                    nc.tensor.transpose(back[:, c, :], held["scaled", b][:, first : first + P], ident)
                 result = tail_pool.tile([P, FEATURES], F32, name="result_%d" % h)
-                nc.vector.tensor_scalar_mul(
-                    out=result, in0=back.rearrange("p c k -> p (c k)"), scalar1=inverse[:, 0:1]
-                )
+                nc.scalar.copy(out=result, in_=back.rearrange("p c k -> p (c k)"))
                 nc.sync.dma_start(out=rows[h], in_=result)
 
-        tail_stages = (variance, deviation, cluster_norm, whole_norm_and_store)
+        tail_stages = (variance, deviation, cluster_norm, whole_norm, store)
 
         pools.enter_context(tc.manual_schedule())
         mu_raw = load_param(mu, "mu")
         sigma_raw = load_param(sigma, "sigma")
-        load_x(0)
         load_probs(0)
-        load_x(1)
+        load_x(0)
         load_probs(1)
-        load_x(2)
-        load_x(3)
+        for u in range(1, LOADS_AHEAD):
+            load_x(u)
         mu_rows = cluster_rows(mu_raw, "mu")
         sigma_rows = cluster_rows(sigma_raw, "sigma")
 
-        for step in range(UNITS + MULTIPLY_LAG + len(tail_stages)):
-            if step < UNITS:
+        last_step = UNITS - 1 + MULTIPLY_LAG + 1 + TAIL_STAGE_GAP * (len(tail_stages) - 1)
+        for step in range(-1, last_step + 1):
+            if 0 <= step < UNITS:
                 flip_x(step)
                 if step + LOADS_AHEAD < UNITS:
                     load_x(step + LOADS_AHEAD)
-            for b in reversed(range(BATCHES)):
-                first = b * BATCH_UNITS
-                last_multiply = first + BATCH_UNITS - 1 + MULTIPLY_LAG
-                for i, stage in enumerate(tail_stages):
-                    if step == last_multiply + 1 + i:
-                        stage(b)
             for b in range(BATCHES):
                 for i, stage in enumerate(p_stages):
-                    if step == max(b * BATCH_UNITS - 2, 0) + i:
+                    if step == max(b * BATCH_UNITS - P_STAGE_LEADS[i], i - 1):
+                        stage(b)
+            for b in reversed(range(BATCHES)):
+                last_multiply = (b + 1) * BATCH_UNITS - 1 + MULTIPLY_LAG
+                for i, stage in enumerate(tail_stages):
+                    if step == last_multiply + 1 + TAIL_STAGE_GAP * i:
                         stage(b)
             if MULTIPLY_LAG <= step < UNITS + MULTIPLY_LAG:
                 multiply(step - MULTIPLY_LAG)
-            if step < UNITS:
+            if 0 <= step < UNITS:
                 square_and_quantise_x(step)

@@ -236,7 +236,6 @@ def tile_wassvladlayer_pb_kernel(tc, probs, x, mu, sigma, out):
 
         tail_stages = (variance, deviation, cluster_norm, whole_norm, store)
 
-        pools.enter_context(tc.manual_schedule())
         mu_raw = load_param(mu, "mu")
         sigma_raw = load_param(sigma, "sigma")
         load_probs(0)

@@ -27,7 +27,7 @@ BATCH_UNITS = POINTS // UNIT_POINTS
 UNITS = BATCHES * BATCH_UNITS
 LOADS_AHEAD = 4
 MULTIPLY_LAG = 2
-VECTOR_SQUARES = UNIT_VALUES * 5 // 8
+SCALAR_SQUARES = UNIT_VALUES * 3 // 8
 P_STAGE_LEADS = (4, 2, 1)
 TAIL_STAGE_GAP = 2
 
@@ -64,7 +64,12 @@ def tile_wassvladlayer_pb_kernel(tc, probs, x, mu, sigma, out):
             b, j = divmod(u, BATCH_UNITS)
             raw = x_pool.tile([P, CHUNKS, UNIT_POINTS], BF16, name="x_raw")
             rows = x[b].rearrange("(p c) n -> p c n", c=CHUNKS)
-            nc.sync.dma_start(out=raw, in_=rows[:, :, j * UNIT_POINTS : (j + 1) * UNIT_POINTS])
+            piece = PASS_POINTS if u == 0 else UNIT_POINTS
+            for first in range(0, UNIT_POINTS, piece):
+                nc.sync.dma_start(
+                    out=raw[:, :, first : first + piece],
+                    in_=rows[:, :, j * UNIT_POINTS + first : j * UNIT_POINTS + first + piece],
+                )
             held["x_raw", u] = raw
 
         def load_param(param, name):
@@ -137,10 +142,10 @@ def tile_wassvladlayer_pb_kernel(tc, probs, x, mu, sigma, out):
         def square_and_quantise_x(u):
             grouped = held["x_grouped", u]
             squares = grouped_pool.tile([P, UNIT_VALUES], BF16, name="sq_grouped", align_bytes=64)
-            mine = slice(0, VECTOR_SQUARES)
-            rest = slice(VECTOR_SQUARES, UNIT_VALUES)
-            nc.vector.tensor_tensor(out=squares[:, mine], in0=grouped[:, mine], in1=grouped[:, mine], op=ALU.mult)
-            nc.scalar.activation(out=squares[:, rest], in_=grouped[:, rest], func=ACT.Square)
+            early = slice(0, SCALAR_SQUARES)
+            late = slice(SCALAR_SQUARES, UNIT_VALUES)
+            nc.scalar.activation(out=squares[:, early], in_=grouped[:, early], func=ACT.Square)
+            nc.vector.tensor_tensor(out=squares[:, late], in0=grouped[:, late], in1=grouped[:, late], op=ALU.mult)
             held["x_mx", u] = quantise(codes_pool, grouped, "x")
             held["sq_mx", u] = quantise(codes_pool, squares, "sq")
 
@@ -169,10 +174,10 @@ def tile_wassvladlayer_pb_kernel(tc, probs, x, mu, sigma, out):
         def variance(b):
             m1_squared = tail_pool.tile([P, FEATURES], F32, name="m1_squared")
             nc.scalar.activation(out=m1_squared, in_=held["m1", b], func=ACT.Square)
-            feat = tail_pool.tile([P, 2 * FEATURES], F32, name="feat")
-            nc.vector.tensor_tensor(out=feat[:, :FEATURES], in0=held["m1", b], in1=mu_rows, op=ALU.subtract)
             spread = tail_pool.tile([P, FEATURES], F32, name="spread")
             nc.vector.tensor_tensor(out=spread, in0=held["m2", b], in1=m1_squared, op=ALU.subtract)
+            feat = tail_pool.tile([P, 2 * FEATURES], F32, name="feat")
+            nc.vector.tensor_tensor(out=feat[:, :FEATURES], in0=held["m1", b], in1=mu_rows, op=ALU.subtract)
             nc.vector.tensor_scalar_max(out=spread, in0=spread, scalar1=EPS)
             held["spread", b] = spread
             held["feat", b] = feat
@@ -195,12 +200,14 @@ def tile_wassvladlayer_pb_kernel(tc, probs, x, mu, sigma, out):
             nc.scalar.activation(out=norm, in_=energy, func=ACT.Sqrt, bias=held["mean_energy", b][:, 0:1])
             floored = tail_pool.tile([P, 1], F32, name="floored")
             nc.vector.tensor_scalar_max(out=floored, in0=norm, scalar1=EPS)
+            left = tail_pool.tile([P, 1], F32, name="left")
+            nc.vector.tensor_scalar(out=left, in0=norm, scalar1=1.0 / EPS, scalar2=1.0, op0=ALU.mult, op1=ALU.min)
             inverse = tail_pool.tile([P, 1], F32, name="inverse")
             nc.vector.reciprocal(out=inverse, in_=floored)
-            left = tail_pool.tile([P, 1], F32, name="left")
-            nc.vector.tensor_tensor(out=left, in0=norm, in1=inverse, op=ALU.mult)
-            held["inverse", b] = inverse
+            scaled = tail_pool.tile([P, 2 * FEATURES], F32, name="scaled")
+            nc.vector.tensor_scalar_mul(out=scaled, in0=held["feat", b], scalar1=inverse[:, 0:1])
             held["left", b] = left
+            held["scaled", b] = scaled
 
         def whole_norm(b):
             left = held["left", b]
@@ -212,16 +219,7 @@ def tile_wassvladlayer_pb_kernel(tc, probs, x, mu, sigma, out):
             nc.vector.tensor_scalar_max(out=floored, in0=norm, scalar1=EPS)
             inverse = tail_pool.tile([P, 1], F32, name="whole_inverse")
             nc.vector.reciprocal(out=inverse, in_=floored)
-            scaled = tail_pool.tile([P, 2 * FEATURES], F32, name="scaled")
-            nc.vector.tensor_scalar(
-                out=scaled,
-                in0=held["feat", b],
-                scalar1=held["inverse", b][:, 0:1],
-                scalar2=inverse[:, 0:1],
-                op0=ALU.mult,
-                op1=ALU.mult,
-            )
-            held["scaled", b] = scaled
+            held["whole_inverse", b] = inverse
 
         def store(b):
             rows = out[b].rearrange("(h p ck) -> h p ck", h=2, p=P)
@@ -231,18 +229,24 @@ def tile_wassvladlayer_pb_kernel(tc, probs, x, mu, sigma, out):
                     first = (h * CHUNKS + c) * P
                     nc.tensor.transpose(back[:, c, :], held["scaled", b][:, first : first + P], ident)
                 result = tail_pool.tile([P, FEATURES], F32, name="result_%d" % h)
-                nc.scalar.copy(out=result, in_=back.rearrange("p c k -> p (c k)"))
+                nc.scalar.activation(
+                    out=result,
+                    in_=back.rearrange("p c k -> p (c k)"),
+                    func=ACT.Copy,
+                    scale=held["whole_inverse", b][:, 0:1],
+                )
                 nc.sync.dma_start(out=rows[h], in_=result)
 
         tail_stages = (variance, deviation, cluster_norm, whole_norm, store)
 
         mu_raw = load_param(mu, "mu")
         sigma_raw = load_param(sigma, "sigma")
-        load_probs(0)
         load_x(0)
+        load_probs(0)
+        load_x(1)
+        load_x(2)
         load_probs(1)
-        for u in range(1, LOADS_AHEAD):
-            load_x(u)
+        load_x(3)
         mu_rows = cluster_rows(mu_raw, "mu")
         sigma_rows = cluster_rows(sigma_raw, "sigma")
 

@@ -25,6 +25,7 @@ UNIT_POINTS = UNIT_PASSES * PASS_POINTS
 UNIT_VALUES = CHUNKS * UNIT_POINTS
 BATCH_UNITS = POINTS // UNIT_POINTS
 UNITS = BATCHES * BATCH_UNITS
+HALF_POINTS = POINTS // 2
 LOADS_AHEAD = 4
 MULTIPLY_LAG = 2
 SCALAR_SQUARES = UNIT_VALUES * 3 // 8
@@ -57,7 +58,9 @@ def tile_wassvladlayer_pb_kernel(tc, probs, x, mu, sigma, out):
 
         def load_probs(b):
             raw = p_raw_pool.tile([P, POINTS], BF16, name="p_raw")
-            nc.sync.dma_start(out=raw, in_=probs[b])
+            for half in range(2):
+                cols = slice(half * HALF_POINTS, (half + 1) * HALF_POINTS)
+                nc.sync.dma_start(out=raw[:, cols], in_=probs[b][:, cols])
             held["p_raw", b] = raw
 
         def load_x(u):
@@ -108,10 +111,20 @@ def tile_wassvladlayer_pb_kernel(tc, probs, x, mu, sigma, out):
         def normalise_p(b):
             raw = held["p_raw", b]
             p_rows = p_pool.tile([P, POINTS], BF16, name="p_rows")
-            total = p_pool.tile([P, 1], F32, name="p_total")
-            nc.vector.tensor_scalar(
-                out=p_rows, in0=raw, scalar1=1.0, scalar2=EPS, op0=ALU.mult, op1=ALU.add, accum_out=total
-            )
+            total = EPS
+            for half in range(2):
+                cols = slice(half * HALF_POINTS, (half + 1) * HALF_POINTS)
+                so_far = total
+                total = p_pool.tile([P, 1], F32, name="p_total_%d" % half)
+                nc.vector.tensor_scalar(
+                    out=p_rows[:, cols],
+                    in0=raw[:, cols],
+                    scalar1=1.0,
+                    scalar2=so_far,
+                    op0=ALU.mult,
+                    op1=ALU.add,
+                    accum_out=total,
+                )
             share = p_pool.tile([P, 1], F32, name="p_share")
             nc.vector.reciprocal(out=share, in_=total)
             nc.vector.tensor_scalar_mul(out=p_rows, in0=raw, scalar1=share[:, 0:1])
@@ -241,8 +254,8 @@ def tile_wassvladlayer_pb_kernel(tc, probs, x, mu, sigma, out):
 
         mu_raw = load_param(mu, "mu")
         sigma_raw = load_param(sigma, "sigma")
-        load_x(0)
         load_probs(0)
+        load_x(0)
         load_x(1)
         load_x(2)
         load_probs(1)

@@ -20,17 +20,19 @@ PASS_POINTS = 4 * P
 PASS_WORDS = PASS_POINTS // 2
 PASSES = POINTS // PASS_POINTS
 CHUNKS = FEATURES // P
-UNIT_PASSES = 2
-UNIT_POINTS = UNIT_PASSES * PASS_POINTS
-UNIT_VALUES = CHUNKS * UNIT_POINTS
-BATCH_UNITS = POINTS // UNIT_POINTS
-UNITS = BATCHES * BATCH_UNITS
 HALF_POINTS = POINTS // 2
+HALF_FEATURES = FEATURES // 2
+UNIT_CHUNKS, UNIT_PASSES = CHUNKS // 2, PASSES // 2
+UNIT_VALUES = UNIT_CHUNKS * HALF_POINTS
+BATCH_UNITS = 4
+UNITS = BATCHES * BATCH_UNITS
+BLOCKS_A_BANK = 2
+BANKS = UNIT_VALUES // 2 // 512
 LOADS_AHEAD = 4
-MULTIPLY_LAG = 2
 SCALAR_SQUARES = UNIT_VALUES * 3 // 8
-P_STAGE_LEADS = (4, 2, 1)
-TAIL_STAGE_GAP = 2
+EARLY_UNITS = 4
+EARLY_SCALAR_SQUARES = UNIT_VALUES * 5 // 8
+LAST_SCALAR_SQUARES = UNIT_VALUES // 2
 
 
 def tile_wassvladlayer_pb_kernel(tc, probs, x, mu, sigma, out):
@@ -39,68 +41,61 @@ def tile_wassvladlayer_pb_kernel(tc, probs, x, mu, sigma, out):
         consts = pools.enter_context(tc.tile_pool(name="consts", bufs=1))
         x_pool = pools.enter_context(tc.tile_pool(name="x_pool", bufs=LOADS_AHEAD))
         p_raw_pool = pools.enter_context(tc.tile_pool(name="p_raw_pool", bufs=2))
-        p_pool = pools.enter_context(tc.tile_pool(name="p_pool", bufs=1))
+        p_pool = pools.enter_context(tc.tile_pool(name="p_pool", bufs=2))
         p_codes_pool = pools.enter_context(tc.tile_pool(name="p_codes_pool", bufs=2))
         grouped_pool = pools.enter_context(tc.tile_pool(name="grouped_pool", bufs=3))
-        codes_pool = pools.enter_context(tc.tile_pool(name="codes_pool", bufs=MULTIPLY_LAG + 2))
+        codes_pool = pools.enter_context(tc.tile_pool(name="codes_pool", bufs=3))
         tail_pool = pools.enter_context(tc.tile_pool(name="tail_pool", bufs=2))
         flip_psum = pools.enter_context(tc.psum_pool(name="flip_psum", bufs=4))
         acc_psum = pools.enter_context(tc.psum_pool(name="acc_psum", bufs=2))
+        pools.enter_context(tc.manual_schedule())
 
         held = {}
 
-        ident = consts.tile([P, P], F32, name="ident")
-        make_identity(nc, ident)
-        one = consts.tile([P, 1], F32, name="one")
-        nc.vector.memset(one, 1.0)
-        root_of_one = consts.tile([P, 1], F32, name="root_of_one")
-        nc.scalar.activation(out=root_of_one, in_=one, func=ACT.Sqrt)
+        def load_probs_half(b, half):
+            if half == 0:
+                held["p_raw", b] = p_raw_pool.tile([P, POINTS], BF16, name="p_raw")
+            cols = slice(half * HALF_POINTS, (half + 1) * HALF_POINTS)
+            nc.sync.dma_start(out=held["p_raw", b][:, cols], in_=probs[b][:, cols])
 
         def load_probs(b):
-            raw = p_raw_pool.tile([P, POINTS], BF16, name="p_raw")
             for half in range(2):
-                cols = slice(half * HALF_POINTS, (half + 1) * HALF_POINTS)
-                nc.sync.dma_start(out=raw[:, cols], in_=probs[b][:, cols])
-            held["p_raw", b] = raw
+                load_probs_half(b, half)
 
-        def load_x(u):
-            b, j = divmod(u, BATCH_UNITS)
-            raw = x_pool.tile([P, CHUNKS, UNIT_POINTS], BF16, name="x_raw")
+        def load_x(u, first=0, points=HALF_POINTS):
+            b, part = divmod(u, BATCH_UNITS)
+            half_f, half_n = divmod(part, 2)
+            if first == 0:
+                held["x_raw", u] = x_pool.tile([P, UNIT_CHUNKS, HALF_POINTS], BF16, name="x_raw")
             rows = x[b].rearrange("(p c) n -> p c n", c=CHUNKS)
-            piece = PASS_POINTS if u == 0 else UNIT_POINTS
-            for first in range(0, UNIT_POINTS, piece):
-                nc.sync.dma_start(
-                    out=raw[:, :, first : first + piece],
-                    in_=rows[:, :, j * UNIT_POINTS + first : j * UNIT_POINTS + first + piece],
-                )
-            held["x_raw", u] = raw
+            start = half_n * HALF_POINTS + first
+            nc.sync.dma_start(
+                out=held["x_raw", u][:, :, first : first + points],
+                in_=rows[:, half_f * UNIT_CHUNKS : (half_f + 1) * UNIT_CHUNKS, start : start + points],
+            )
 
         def load_param(param, name):
             raw = consts.tile([P, CHUNKS, CLUSTERS], BF16, name=name + "_raw")
-            nc.scalar.dma_start(out=raw, in_=param[0].rearrange("(p c) k -> p c k", c=CHUNKS))
+            nc.sync.dma_start(out=raw, in_=param[0].rearrange("(p c) k -> p c k", c=CHUNKS))
             return raw
 
         def cluster_rows(raw, name):
-            wide = consts.tile([P, CHUNKS, CLUSTERS], F32, name=name + "_wide")
-            nc.vector.tensor_copy(out=wide, in_=raw)
-            back = flip_psum.tile([P, CHUNKS, P], F32, name="param_back", tag="flipped")
+            back = flip_psum.tile([P, CHUNKS, P], BF16, name="param_back", tag="flipped")
             for c in range(CHUNKS):
-                nc.tensor.transpose(back[:, c, :], wide[:, c, :], ident)
-            rows = consts.tile([P, FEATURES], F32, name=name + "_rows")
+                nc.tensor.transpose(back[:, c, :], raw[:, c, :], ident_bf16)
+            rows = consts.tile([P, FEATURES], BF16, name=name + "_rows")
             nc.scalar.copy(out=rows, in_=back.rearrange("p c d -> p (c d)"))
-            return rows
+            held[name] = rows
 
-        def points_onto_partitions(blocks_of_words, grouped):
-            grouped_words = grouped.bitcast(F32).rearrange("q (blk row half) -> q blk row half", row=P, half=2)
-            for first in range(0, len(blocks_of_words), 2):
-                flipped = flip_psum.tile([P, 2, 2, P], F32, name="flipped")
-                for i in range(2):
-                    words = blocks_of_words[first + i]
-                    for half in range(2):
-                        nc.tensor.transpose(flipped[:, i, half, :], words[:, half * P : (half + 1) * P], ident)
-                nc.scalar.copy(
-                    out=grouped_words[:, first : first + 2], in_=flipped.rearrange("q i half row -> q i row half")
-                )
+        def flip_bank(blocks, grouped_words, copy):
+            flipped = flip_psum.tile([P, BLOCKS_A_BANK, 2, P], F32, name="flipped")
+            for i, words in enumerate(blocks):
+                for half in range(2):
+                    nc.tensor.transpose(flipped[:, i, half, :], words[:, half * P : (half + 1) * P], ident)
+            copy(out=grouped_words, in_=flipped.rearrange("q i half row -> q i row half"))
+
+        def word_blocks(grouped):
+            return grouped.bitcast(F32).rearrange("q (blk row half) -> q blk row half", row=P, half=2)
 
         def quantise(pool, grouped, name):
             codes = pool.tile([P, UNIT_VALUES // 4], U32, name=name + "_codes", align_bytes=64)
@@ -108,177 +103,367 @@ def tile_wassvladlayer_pb_kernel(tc, probs, x, mu, sigma, out):
             nc.vector.quantize_mx(out=codes.bitcast(FP8X4), scales=scales, in_=grouped)
             return codes, scales
 
-        def normalise_p(b):
-            raw = held["p_raw", b]
-            p_rows = p_pool.tile([P, POINTS], BF16, name="p_rows")
-            total = EPS
-            for half in range(2):
-                cols = slice(half * HALF_POINTS, (half + 1) * HALF_POINTS)
-                so_far = total
-                total = p_pool.tile([P, 1], F32, name="p_total_%d" % half)
-                nc.vector.tensor_scalar(
-                    out=p_rows[:, cols],
-                    in0=raw[:, cols],
-                    scalar1=1.0,
-                    scalar2=so_far,
-                    op0=ALU.mult,
-                    op1=ALU.add,
-                    accum_out=total,
-                )
-            share = p_pool.tile([P, 1], F32, name="p_share")
-            nc.vector.reciprocal(out=share, in_=total)
-            nc.vector.tensor_scalar_mul(out=p_rows, in0=raw, scalar1=share[:, 0:1])
-            held["p_rows", b] = p_rows
-            if b + 2 < BATCHES:
-                load_probs(b + 2)
+        def sum_p(b, half):
+            if half == 0:
+                held["p_rows", b] = p_pool.tile([P, POINTS], BF16, name="p_rows")
+            cols = slice(half * HALF_POINTS, (half + 1) * HALF_POINTS)
+            so_far = held["p_total", b] if half else EPS
+            total = p_pool.tile([P, 1], F32, name="p_total_%d" % half)
+            nc.vector.tensor_scalar(
+                out=held["p_rows", b][:, cols],
+                in0=held["p_raw", b][:, cols],
+                scalar1=1.0,
+                scalar2=so_far,
+                op0=ALU.mult,
+                op1=ALU.add,
+                accum_out=total,
+            )
+            held["p_total", b] = total
 
-        def flip_p(b):
+        def invert_p(b):
+            held["p_share", b] = p_pool.tile([P, 1], F32, name="p_share")
+            nc.vector.reciprocal(out=held["p_share", b], in_=held["p_total", b])
+
+        def scale_p(b):
+            nc.vector.tensor_scalar_mul(
+                out=held["p_rows", b], in0=held["p_raw", b], scalar1=held["p_share", b][:, 0:1]
+            )
+
+        def flip_p(b, bank):
+            if bank == 0:
+                held["p_grouped", b] = p_pool.tile([P, POINTS], BF16, name="p_grouped", align_bytes=64)
             words = held["p_rows", b].bitcast(F32)
-            grouped = p_pool.tile([P, UNIT_VALUES], BF16, name="p_grouped", align_bytes=64)
-            points_onto_partitions([words[:, g * PASS_WORDS : (g + 1) * PASS_WORDS] for g in range(PASSES)], grouped)
-            held["p_grouped", b] = grouped
+            passes = range(bank * BLOCKS_A_BANK, (bank + 1) * BLOCKS_A_BANK)
+            flip_bank(
+                [words[:, g * PASS_WORDS : (g + 1) * PASS_WORDS] for g in passes],
+                word_blocks(held["p_grouped", b])[:, bank * BLOCKS_A_BANK : (bank + 1) * BLOCKS_A_BANK],
+                nc.vector.tensor_copy if b == 0 else nc.scalar.copy,
+            )
 
         def quantise_p(b):
             held["p_mx", b] = quantise(p_codes_pool, held["p_grouped", b], "p")
 
-        p_stages = (normalise_p, flip_p, quantise_p)
-
-        def flip_x(u):
+        def flip_x(u, first=0, stop=UNIT_PASSES):
+            if first == 0:
+                held["x_grouped", u] = grouped_pool.tile([P, UNIT_VALUES], BF16, name="x_grouped", align_bytes=64)
             words = held["x_raw", u].bitcast(F32)
-            grouped = grouped_pool.tile([P, UNIT_VALUES], BF16, name="x_grouped", align_bytes=64)
-            points_onto_partitions(
-                [words[:, c, g * PASS_WORDS : (g + 1) * PASS_WORDS] for g in range(UNIT_PASSES) for c in range(CHUNKS)],
-                grouped,
-            )
-            held["x_grouped", u] = grouped
+            for g in range(first, stop):
+                flip_bank(
+                    [words[:, c, g * PASS_WORDS : (g + 1) * PASS_WORDS] for c in range(UNIT_CHUNKS)],
+                    word_blocks(held["x_grouped", u])[:, g * UNIT_CHUNKS : (g + 1) * UNIT_CHUNKS],
+                    nc.scalar.copy,
+                )
 
-        def square_and_quantise_x(u):
-            grouped = held["x_grouped", u]
-            squares = grouped_pool.tile([P, UNIT_VALUES], BF16, name="sq_grouped", align_bytes=64)
-            early = slice(0, SCALAR_SQUARES)
-            late = slice(SCALAR_SQUARES, UNIT_VALUES)
-            nc.scalar.activation(out=squares[:, early], in_=grouped[:, early], func=ACT.Square)
-            nc.vector.tensor_tensor(out=squares[:, late], in0=grouped[:, late], in1=grouped[:, late], op=ALU.mult)
-            held["x_mx", u] = quantise(codes_pool, grouped, "x")
-            held["sq_mx", u] = quantise(codes_pool, squares, "sq")
+        def scalar_share(u):
+            if u == 0:
+                return UNIT_VALUES // 2
+            if u == UNITS - 1:
+                return LAST_SCALAR_SQUARES
+            return EARLY_SCALAR_SQUARES if u < EARLY_UNITS else SCALAR_SQUARES
 
-        def multiply(u):
-            b, j = divmod(u, BATCH_UNITS)
-            if j == 0:
-                held["m1", b] = acc_psum.tile([P, FEATURES], F32, name="m1")
-                held["m2", b] = acc_psum.tile([P, FEATURES], F32, name="m2")
+        def square_scalar(u):
+            held["squares", u] = grouped_pool.tile([P, UNIT_VALUES], BF16, name="sq_grouped", align_bytes=64)
+            part = slice(0, scalar_share(u))
+            nc.scalar.activation(out=held["squares", u][:, part], in_=held["x_grouped", u][:, part], func=ACT.Square)
+
+        def square_vector(u):
+            part = slice(scalar_share(u), UNIT_VALUES)
+            if part.start < part.stop:
+                values = held["x_grouped", u][:, part]
+                nc.vector.tensor_tensor(out=held["squares", u][:, part], in0=values, in1=values, op=ALU.mult)
+
+        def quantise_x(u):
+            held["x_mx", u] = quantise(codes_pool, held["x_grouped", u], "x")
+
+        def quantise_squares(u):
+            held["sq_mx", u] = quantise(codes_pool, held["squares", u], "sq")
+
+        def acc_key(b, half_f):
+            return (b, half_f if b == BATCHES - 1 else 0)
+
+        def multiply(u, moment, operand):
+            b, part = divmod(u, BATCH_UNITS)
+            half_f, half_n = divmod(part, 2)
+            key = (moment, acc_key(b, half_f))
+            if key not in held:
+                held[key] = acc_psum.tile([P, FEATURES], F32, name=moment)
+            acc = held[key][:, half_f * HALF_FEATURES : (half_f + 1) * HALF_FEATURES]
             p_codes, p_scales = held["p_mx", b]
-            for acc, operand in (("m1", "x_mx"), ("m2", "sq_mx")):
-                codes, scales = held[operand, u]
-                for g in range(UNIT_PASSES):
-                    whole = j * UNIT_PASSES + g
-                    p_cols = slice(whole * CLUSTERS, (whole + 1) * CLUSTERS)
-                    x_cols = slice(g * FEATURES, (g + 1) * FEATURES)
-                    nc.tensor.matmul_mx(
-                        out=held[acc, b],
-                        lhsT=p_codes[:, p_cols].bitcast(FP8X4),
-                        lhsT_scale=p_scales[:, p_cols],
-                        rhs=codes[:, x_cols].bitcast(FP8X4),
-                        rhs_scale=scales[:, x_cols],
-                        start=(whole == 0),
-                        stop=(whole == PASSES - 1),
-                    )
+            codes, scales = held[operand, u]
+            for g in range(UNIT_PASSES):
+                whole = half_n * UNIT_PASSES + g
+                p_cols = slice(whole * CLUSTERS, (whole + 1) * CLUSTERS)
+                x_cols = slice(g * HALF_FEATURES, (g + 1) * HALF_FEATURES)
+                nc.tensor.matmul_mx(
+                    out=acc,
+                    lhsT=p_codes[:, p_cols].bitcast(FP8X4),
+                    lhsT_scale=p_scales[:, p_cols],
+                    rhs=codes[:, x_cols].bitcast(FP8X4),
+                    rhs_scale=scales[:, x_cols],
+                    start=(whole == 0),
+                    stop=(whole == PASSES - 1),
+                )
 
-        def variance(b):
-            m1_squared = tail_pool.tile([P, FEATURES], F32, name="m1_squared")
-            nc.scalar.activation(out=m1_squared, in_=held["m1", b], func=ACT.Square)
-            spread = tail_pool.tile([P, FEATURES], F32, name="spread")
-            nc.vector.tensor_tensor(out=spread, in0=held["m2", b], in1=m1_squared, op=ALU.subtract)
-            feat = tail_pool.tile([P, 2 * FEATURES], F32, name="feat")
-            nc.vector.tensor_tensor(out=feat[:, :FEATURES], in0=held["m1", b], in1=mu_rows, op=ALU.subtract)
+        ALL = slice(0, FEATURES)
+        HALVES = (slice(0, HALF_FEATURES), slice(HALF_FEATURES, FEATURES))
+
+        def moment_tile(moment, b, cols):
+            return held[moment, acc_key(b, 0 if cols.start == 0 else 1)][:, cols]
+
+        def tail_tile(what, b, width):
+            if (what, b) not in held:
+                held[what, b] = tail_pool.tile([P, width], F32, name=what)
+            return held[what, b]
+
+        def feat_tile(b, h, cols):
+            return tail_tile("feat", b, 2 * FEATURES)[:, h * FEATURES + cols.start : h * FEATURES + cols.stop]
+
+        def square_m1(b, cols):
+            nc.scalar.activation(
+                out=tail_tile("m1_squared", b, FEATURES)[:, cols], in_=moment_tile("m1", b, cols), func=ACT.Square
+            )
+
+        def mean_residual(b, cols):
+            nc.vector.tensor_tensor(
+                out=feat_tile(b, 0, cols), in0=moment_tile("m1", b, cols), in1=held["mu"][:, cols], op=ALU.subtract
+            )
+
+        def variance(b, cols):
+            nc.vector.tensor_tensor(
+                out=tail_tile("spread", b, FEATURES)[:, cols],
+                in0=moment_tile("m2", b, cols),
+                in1=held["m1_squared", b][:, cols],
+                op=ALU.subtract,
+            )
+
+        def floor_variance(b, cols):
+            spread = held["spread", b][:, cols]
             nc.vector.tensor_scalar_max(out=spread, in0=spread, scalar1=EPS)
-            held["spread", b] = spread
-            held["feat", b] = feat
 
-        def deviation(b):
-            feat = held["feat", b]
-            sigma_hat = tail_pool.tile([P, FEATURES], F32, name="sigma_hat")
-            nc.scalar.activation(out=sigma_hat, in_=held["spread", b], func=ACT.Sqrt)
-            unread = tail_pool.tile([P, FEATURES], F32, name="unread_mean")
-            energy = tail_pool.tile([P, 1], F32, name="mean_energy")
-            nc.scalar.activation(out=unread, in_=feat[:, :FEATURES], func=ACT.Square, accum_out=energy)
-            nc.vector.tensor_tensor(out=feat[:, FEATURES:], in0=sigma_hat, in1=sigma_rows, op=ALU.subtract)
-            held["mean_energy", b] = energy
+        def deviation(b, cols):
+            nc.scalar.activation(
+                out=tail_tile("deviation", b, FEATURES)[:, cols], in_=held["spread", b][:, cols], func=ACT.Sqrt
+            )
+
+        def deviation_residual(b, cols):
+            nc.vector.tensor_tensor(
+                out=feat_tile(b, 1, cols), in0=held["deviation", b][:, cols], in1=held["sigma"][:, cols], op=ALU.subtract
+            )
+
+        def add_squares(b, first, stop, column):
+            unread = tail_tile("unread", b, 2 * FEATURES)[:, first:stop]
+            energy = tail_tile("energies", b, 4)[:, column : column + 1]
+            nc.scalar.activation(out=unread, in_=held["feat", b][:, first:stop], func=ACT.Square, accum_out=energy)
+
+        def add_energies(b):
+            nc.vector.reduce_sum(out=tail_tile("energy", b, 1), in_=held["energies", b], axis=mybir.AxisListType.X)
 
         def cluster_norm(b):
-            unread = tail_pool.tile([P, FEATURES], F32, name="unread_deviation")
-            energy = tail_pool.tile([P, 1], F32, name="deviation_energy")
-            nc.scalar.activation(out=unread, in_=held["feat", b][:, FEATURES:], func=ACT.Square, accum_out=energy)
-            norm = tail_pool.tile([P, 1], F32, name="norm")
-            nc.scalar.activation(out=norm, in_=energy, func=ACT.Sqrt, bias=held["mean_energy", b][:, 0:1])
-            floored = tail_pool.tile([P, 1], F32, name="floored")
-            nc.vector.tensor_scalar_max(out=floored, in0=norm, scalar1=EPS)
-            left = tail_pool.tile([P, 1], F32, name="left")
-            nc.vector.tensor_scalar(out=left, in0=norm, scalar1=1.0 / EPS, scalar2=1.0, op0=ALU.mult, op1=ALU.min)
-            inverse = tail_pool.tile([P, 1], F32, name="inverse")
-            nc.vector.reciprocal(out=inverse, in_=floored)
-            scaled = tail_pool.tile([P, 2 * FEATURES], F32, name="scaled")
-            nc.vector.tensor_scalar_mul(out=scaled, in0=held["feat", b], scalar1=inverse[:, 0:1])
-            held["left", b] = left
-            held["scaled", b] = scaled
+            energy = held["energy", b] if b == BATCHES - 1 else held["energies", b][:, 0:1]
+            nc.scalar.activation(out=tail_tile("norm", b, 1), in_=energy, func=ACT.Sqrt)
+
+        def norm_left(b):
+            nc.vector.tensor_scalar(
+                out=tail_tile("left", b, 1), in0=held["norm", b], scalar1=1.0 / EPS, scalar2=1.0, op0=ALU.mult, op1=ALU.min
+            )
+
+        def norm_floor(b):
+            nc.vector.tensor_scalar_max(out=tail_tile("floored", b, 1), in0=held["norm", b], scalar1=EPS)
+
+        def norm_invert(b):
+            nc.vector.reciprocal(out=tail_tile("inverse", b, 1), in_=held["floored", b])
+
+        def scale_columns(b, h):
+            cols = slice(h * FEATURES, (h + 1) * FEATURES)
+            nc.vector.tensor_scalar_mul(
+                out=tail_tile("scaled", b, 2 * FEATURES)[:, cols], in0=held["feat", b][:, cols], scalar1=held["inverse", b][:, 0:1]
+            )
+
+        def add_left(b):
+            held["whole", b] = flip_psum.tile([P, 1], F32, name="whole", tag="flipped")
+            left = held["left", b]
+            nc.tensor.matmul(out=held["whole", b], lhsT=left[:, 0:1].to_broadcast([P, P]), rhs=left, start=True, stop=True)
 
         def whole_norm(b):
-            left = held["left", b]
-            whole = flip_psum.tile([P, 1], F32, name="whole", tag="flipped")
-            nc.tensor.matmul(out=whole, lhsT=left[:, 0:1].to_broadcast([P, P]), rhs=left, start=True, stop=True)
-            norm = tail_pool.tile([P, 1], F32, name="whole_norm")
-            nc.scalar.activation(out=norm, in_=whole, func=ACT.Sqrt)
-            floored = tail_pool.tile([P, 1], F32, name="whole_floored")
-            nc.vector.tensor_scalar_max(out=floored, in0=norm, scalar1=EPS)
-            inverse = tail_pool.tile([P, 1], F32, name="whole_inverse")
-            nc.vector.reciprocal(out=inverse, in_=floored)
-            held["whole_inverse", b] = inverse
+            nc.scalar.activation(out=tail_tile("whole_norm", b, 1), in_=held["whole", b], func=ACT.Sqrt)
 
-        def store(b):
+        def whole_floor(b):
+            nc.vector.tensor_scalar_max(out=tail_tile("whole_floored", b, 1), in0=held["whole_norm", b], scalar1=EPS)
+
+        def whole_invert(b):
+            nc.vector.reciprocal(out=tail_tile("whole_inverse", b, 1), in_=held["whole_floored", b])
+
+        def turn_back(b, h):
+            held["back", b, h] = flip_psum.tile([P, CHUNKS, P], F32, name="back", tag="flipped")
+            for c in range(CHUNKS):
+                first = h * FEATURES + c * P
+                nc.tensor.transpose(held["back", b, h][:, c, :], held["scaled", b][:, first : first + P], ident)
+
+        def store(b, h, on_vector=False):
             rows = out[b].rearrange("(h p ck) -> h p ck", h=2, p=P)
-            for h in range(2):
-                back = flip_psum.tile([P, CHUNKS, P], F32, name="back", tag="flipped")
-                for c in range(CHUNKS):
-                    first = (h * CHUNKS + c) * P
-                    nc.tensor.transpose(back[:, c, :], held["scaled", b][:, first : first + P], ident)
-                result = tail_pool.tile([P, FEATURES], F32, name="result_%d" % h)
-                nc.scalar.activation(
-                    out=result,
-                    in_=back.rearrange("p c k -> p (c k)"),
-                    func=ACT.Copy,
-                    scale=held["whole_inverse", b][:, 0:1],
-                )
-                nc.sync.dma_start(out=rows[h], in_=result)
+            result = tail_pool.tile([P, FEATURES], F32, name="result_%d" % h)
+            back = held["back", b, h].rearrange("p c k -> p (c k)")
+            if on_vector:
+                nc.vector.tensor_scalar_mul(out=result, in0=back, scalar1=held["whole_inverse", b][:, 0:1])
+            else:
+                nc.scalar.activation(out=result, in_=back, func=ACT.Copy, scale=held["whole_inverse", b][:, 0:1])
+            nc.sync.dma_start(out=rows[h], in_=result)
 
-        tail_stages = (variance, deviation, cluster_norm, whole_norm, store)
+        def run(work):
+            for stage, *args in work:
+                stage(*args)
 
+        load_x(0, 0, HALF_POINTS // 2)
+        load_probs_half(0, 0)
+        load_probs_half(0, 1)
+        load_x(0, HALF_POINTS // 2, HALF_POINTS // 2)
+        load_x(1)
+        load_probs(1)
+        load_x(2)
         mu_raw = load_param(mu, "mu")
         sigma_raw = load_param(sigma, "sigma")
-        load_probs(0)
-        load_x(0)
-        load_x(1)
-        load_x(2)
-        load_probs(1)
         load_x(3)
-        mu_rows = cluster_rows(mu_raw, "mu")
-        sigma_rows = cluster_rows(sigma_raw, "sigma")
 
-        last_step = UNITS - 1 + MULTIPLY_LAG + 1 + TAIL_STAGE_GAP * (len(tail_stages) - 1)
-        for step in range(-1, last_step + 1):
-            if 0 <= step < UNITS:
+        ident = consts.tile([P, P], F32, name="ident")
+        make_identity(nc, ident)
+        ident_bf16 = consts.tile([P, P], BF16, name="ident_bf16")
+        make_identity(nc, ident_bf16)
+        one = consts.tile([P, 1], F32, name="one")
+        nc.vector.memset(one, 1.0)
+        root_of_one = consts.tile([P, 1], F32, name="root_of_one")
+        nc.scalar.activation(out=root_of_one, in_=one, func=ACT.Sqrt)
+
+        sum_p(0, 0)
+        sum_p(0, 1)
+        invert_p(0)
+        scale_p(0)
+        for step in range(UNITS):
+            vector_unit = step - 1
+            vec_a, vec_b, vec_c, vec_d, act_first, act_mid, act_last, pe_mid, pe_last = [], [], [], [], [], [], [], [], []
+            if step == UNITS - 1:
+                act_mid.append((square_m1, BATCHES - 1, HALVES[0]))
+            for b in range(1, BATCHES):
+                begin = max(BATCH_UNITS * (b - 1) - 1, 1)
+                if step == begin:
+                    vec_c.append((sum_p, b, 0))
+                if step == begin + 1:
+                    vec_c.append((sum_p, b, 1))
+                    vec_d.append((invert_p, b))
+                if step == begin + 2:
+                    vec_a.append((scale_p, b))
+                for bank in range(BANKS):
+                    if step == max(BATCH_UNITS * b - 3 + bank, begin + 2 + bank // 2):
+                        pe_last.append((flip_p, b, bank))
+                if step == BATCH_UNITS * b + 1:
+                    vec_c.append((quantise_p, b))
+            if step == 1:
+                for bank in range(BANKS):
+                    vec_d.append((flip_p, 0, bank))
+            if step == 2:
+                vec_b.append((quantise_p, 0))
+            if step == 3:
+                pe_last.append((cluster_rows, mu_raw, "mu"))
+                pe_last.append((cluster_rows, sigma_raw, "sigma"))
+            for b in range(BATCHES - 1):
+                phase = step - BATCH_UNITS * (b + 1) - 1
+                if phase == 0:
+                    act_mid.append((square_m1, b, ALL))
+                    vec_c.append((mean_residual, b, ALL))
+                    vec_d.append((variance, b, ALL))
+                elif phase == 1:
+                    vec_a.append((floor_variance, b, ALL))
+                    act_mid.append((deviation, b, ALL))
+                    vec_c.append((deviation_residual, b, ALL))
+                    act_last.append((add_squares, b, 0, 2 * FEATURES, 0))
+                elif phase == 2:
+                    act_first.append((cluster_norm, b))
+                    vec_b.append((norm_left, b))
+                    vec_b.append((norm_floor, b))
+                    vec_c.append((norm_invert, b))
+                    pe_last.append((add_left, b))
+                    vec_d.append((scale_columns, b, 0))
+                    vec_d.append((scale_columns, b, 1))
+                    act_last.append((whole_norm, b))
+                elif phase == 3:
+                    vec_a.append((whole_floor, b))
+                    vec_b.append((whole_invert, b))
+                    pe_mid.append((turn_back, b, 0))
+                    act_last.append((store, b, 0))
+                    pe_last.append((turn_back, b, 1))
+                    act_last.append((store, b, 1))
+
+            run(act_first)
+            if step == 0:
+                flip_x(0, 0, UNIT_PASSES // 2)
+                square_scalar(0)
+                flip_x(0, UNIT_PASSES // 2)
+            else:
                 flip_x(step)
-                if step + LOADS_AHEAD < UNITS:
-                    load_x(step + LOADS_AHEAD)
-            for b in range(BATCHES):
-                for i, stage in enumerate(p_stages):
-                    if step == max(b * BATCH_UNITS - P_STAGE_LEADS[i], i - 1):
-                        stage(b)
-            for b in reversed(range(BATCHES)):
-                last_multiply = (b + 1) * BATCH_UNITS - 1 + MULTIPLY_LAG
-                for i, stage in enumerate(tail_stages):
-                    if step == last_multiply + 1 + TAIL_STAGE_GAP * i:
-                        stage(b)
-            if MULTIPLY_LAG <= step < UNITS + MULTIPLY_LAG:
-                multiply(step - MULTIPLY_LAG)
-            if 0 <= step < UNITS:
-                square_and_quantise_x(step)
+            if step + LOADS_AHEAD < UNITS:
+                load_x(step + LOADS_AHEAD)
+            if step >= 1 and step % BATCH_UNITS == 1 and step // BATCH_UNITS + 2 < BATCHES:
+                load_probs(step // BATCH_UNITS + 2)
+            for u in {2: [], 3: [0, 1]}.get(step, [step - 2]):
+                if u >= 0:
+                    multiply(u, "m1", "x_mx")
+                    multiply(u, "m2", "sq_mx")
+            run(pe_mid)
+            run(vec_a)
+            run(act_mid)
+            if step > 0:
+                square_scalar(step)
+            if vector_unit >= 0:
+                square_vector(vector_unit)
+                run(vec_b)
+                quantise_x(vector_unit)
+                run(vec_c)
+                quantise_squares(vector_unit)
+            run(vec_d)
+            run(pe_last)
+            run(act_last)
+
+        b, last = BATCHES - 1, UNITS - 1
+        first, second = HALVES
+        multiply(last - 1, "m1", "x_mx")
+        multiply(last - 1, "m2", "sq_mx")
+        turn_back(b - 1, 0)
+        turn_back(b - 1, 1)
+        square_vector(last)
+        whole_floor(b - 1)
+        quantise_x(last)
+        whole_invert(b - 1)
+        multiply(last, "m1", "x_mx")
+        mean_residual(b, first)
+        variance(b, first)
+        floor_variance(b, first)
+        square_m1(b, second)
+        quantise_squares(last)
+        multiply(last, "m2", "sq_mx")
+        deviation(b, first)
+        add_squares(b, 0, HALF_FEATURES, 0)
+        mean_residual(b, second)
+        deviation_residual(b, first)
+        variance(b, second)
+        add_squares(b, FEATURES, FEATURES + HALF_FEATURES, 1)
+        floor_variance(b, second)
+        add_squares(b, HALF_FEATURES, FEATURES, 2)
+        deviation(b, second)
+        deviation_residual(b, second)
+        add_squares(b, FEATURES + HALF_FEATURES, 2 * FEATURES, 3)
+        store(b - 1, 0, on_vector=True)
+        add_energies(b)
+        cluster_norm(b)
+        norm_floor(b)
+        norm_left(b)
+        norm_invert(b)
+        store(b - 1, 1)
+        add_left(b)
+        scale_columns(b, 0)
+        turn_back(b, 0)
+        scale_columns(b, 1)
+        turn_back(b, 1)
+        whole_norm(b)
+        whole_floor(b)
+        whole_invert(b)
+        store(b, 0)
+        store(b, 1, on_vector=True)

@@ -31,8 +31,8 @@ BANKS = UNIT_VALUES // 2 // 512
 LOADS_AHEAD = 4
 SCALAR_SQUARES = UNIT_VALUES * 3 // 8
 EARLY_UNITS = 4
-EARLY_SCALAR_SQUARES = UNIT_VALUES * 5 // 8
-LAST_SCALAR_SQUARES = UNIT_VALUES // 2
+EARLY_SCALAR_SQUARES = UNIT_VALUES // 2
+LAST_SCALAR_SQUARES = UNIT_VALUES * 3 // 4
 
 
 def tile_wassvladlayer_pb_kernel(tc, probs, x, mu, sigma, out):
@@ -44,10 +44,10 @@ def tile_wassvladlayer_pb_kernel(tc, probs, x, mu, sigma, out):
         p_pool = pools.enter_context(tc.tile_pool(name="p_pool", bufs=2))
         p_codes_pool = pools.enter_context(tc.tile_pool(name="p_codes_pool", bufs=2))
         grouped_pool = pools.enter_context(tc.tile_pool(name="grouped_pool", bufs=3))
-        codes_pool = pools.enter_context(tc.tile_pool(name="codes_pool", bufs=3))
+        codes_pool = pools.enter_context(tc.tile_pool(name="codes_pool", bufs=4))
         tail_pool = pools.enter_context(tc.tile_pool(name="tail_pool", bufs=2))
-        flip_psum = pools.enter_context(tc.psum_pool(name="flip_psum", bufs=4))
-        acc_psum = pools.enter_context(tc.psum_pool(name="acc_psum", bufs=2))
+        flip_psum = pools.enter_context(tc.psum_pool(name="flip_psum", bufs=6))
+        acc_psum = pools.enter_context(tc.psum_pool(name="acc_psum", bufs=1))
         pools.enter_context(tc.manual_schedule())
 
         held = {}
@@ -66,11 +66,17 @@ def tile_wassvladlayer_pb_kernel(tc, probs, x, mu, sigma, out):
             b, part = divmod(u, BATCH_UNITS)
             half_f, half_n = divmod(part, 2)
             if first == 0:
-                held["x_raw", u] = x_pool.tile([P, UNIT_CHUNKS, HALF_POINTS], BF16, name="x_raw")
+                held["x_raw", u] = x_pool.tile([P, UNIT_VALUES], BF16, name="x_raw")
             rows = x[b].rearrange("(p c) n -> p c n", c=CHUNKS)
             start = half_n * HALF_POINTS + first
+            piece = held["x_raw", u][:, UNIT_CHUNKS * first : UNIT_CHUNKS * (first + points)]
+            piece = piece.rearrange("p (c n) -> p c n", c=UNIT_CHUNKS)
+            words = piece.bitcast(F32)
+            for g in range(points // PASS_POINTS):
+                cols = slice(g * PASS_WORDS, (g + 1) * PASS_WORDS)
+                held["x_words", u, first // PASS_POINTS + g] = [words[:, c, cols] for c in range(UNIT_CHUNKS)]
             nc.sync.dma_start(
-                out=held["x_raw", u][:, :, first : first + points],
+                out=piece,
                 in_=rows[:, half_f * UNIT_CHUNKS : (half_f + 1) * UNIT_CHUNKS, start : start + points],
             )
 
@@ -137,7 +143,7 @@ def tile_wassvladlayer_pb_kernel(tc, probs, x, mu, sigma, out):
             flip_bank(
                 [words[:, g * PASS_WORDS : (g + 1) * PASS_WORDS] for g in passes],
                 word_blocks(held["p_grouped", b])[:, bank * BLOCKS_A_BANK : (bank + 1) * BLOCKS_A_BANK],
-                nc.vector.tensor_copy if b == 0 else nc.scalar.copy,
+                nc.scalar.copy,
             )
 
         def quantise_p(b):
@@ -146,10 +152,9 @@ def tile_wassvladlayer_pb_kernel(tc, probs, x, mu, sigma, out):
         def flip_x(u, first=0, stop=UNIT_PASSES):
             if first == 0:
                 held["x_grouped", u] = grouped_pool.tile([P, UNIT_VALUES], BF16, name="x_grouped", align_bytes=64)
-            words = held["x_raw", u].bitcast(F32)
             for g in range(first, stop):
                 flip_bank(
-                    [words[:, c, g * PASS_WORDS : (g + 1) * PASS_WORDS] for c in range(UNIT_CHUNKS)],
+                    held["x_words", u, g],
                     word_blocks(held["x_grouped", u])[:, g * UNIT_CHUNKS : (g + 1) * UNIT_CHUNKS],
                     nc.scalar.copy,
                 )
@@ -186,7 +191,10 @@ def tile_wassvladlayer_pb_kernel(tc, probs, x, mu, sigma, out):
             half_f, half_n = divmod(part, 2)
             key = (moment, acc_key(b, half_f))
             if key not in held:
-                held[key] = acc_psum.tile([P, FEATURES], F32, name=moment)
+                if u < UNITS - 2:
+                    held[key] = acc_psum.tile([P, FEATURES], F32, name=moment)
+                else:
+                    held[key] = flip_psum.tile([P, FEATURES], F32, name="last_" + moment, tag="flipped")
             acc = held[key][:, half_f * HALF_FEATURES : (half_f + 1) * HALF_FEATURES]
             p_codes, p_scales = held["p_mx", b]
             codes, scales = held[operand, u]
@@ -313,10 +321,11 @@ def tile_wassvladlayer_pb_kernel(tc, probs, x, mu, sigma, out):
             for stage, *args in work:
                 stage(*args)
 
-        load_x(0, 0, HALF_POINTS // 2)
+        load_x(0, 0, PASS_POINTS)
         load_probs_half(0, 0)
+        load_x(0, PASS_POINTS, PASS_POINTS)
         load_probs_half(0, 1)
-        load_x(0, HALF_POINTS // 2, HALF_POINTS // 2)
+        load_x(0, 2 * PASS_POINTS, 2 * PASS_POINTS)
         load_x(1)
         load_probs(1)
         load_x(2)
@@ -339,7 +348,8 @@ def tile_wassvladlayer_pb_kernel(tc, probs, x, mu, sigma, out):
         scale_p(0)
         for step in range(UNITS):
             vector_unit = step - 1
-            vec_a, vec_b, vec_c, vec_d, act_first, act_mid, act_last, pe_mid, pe_last = [], [], [], [], [], [], [], [], []
+            vec_a, vec_b, vec_c, vec_d, vec_e = [], [], [], [], []
+            act_first, act_mid, act_late, act_last, pe_mid, pe_last = [], [], [], [], [], []
             if step == UNITS - 1:
                 act_mid.append((square_m1, BATCHES - 1, HALVES[0]))
             for b in range(1, BATCHES):
@@ -356,9 +366,6 @@ def tile_wassvladlayer_pb_kernel(tc, probs, x, mu, sigma, out):
                         pe_last.append((flip_p, b, bank))
                 if step == BATCH_UNITS * b + 1:
                     vec_c.append((quantise_p, b))
-            if step == 1:
-                for bank in range(BANKS):
-                    vec_d.append((flip_p, 0, bank))
             if step == 2:
                 vec_b.append((quantise_p, 0))
             if step == 3:
@@ -380,13 +387,13 @@ def tile_wassvladlayer_pb_kernel(tc, probs, x, mu, sigma, out):
                     vec_b.append((norm_left, b))
                     vec_b.append((norm_floor, b))
                     vec_c.append((norm_invert, b))
-                    pe_last.append((add_left, b))
+                    pe_mid.append((add_left, b))
                     vec_d.append((scale_columns, b, 0))
                     vec_d.append((scale_columns, b, 1))
-                    act_last.append((whole_norm, b))
+                    act_late.append((whole_norm, b))
+                    vec_e.append((whole_floor, b))
+                    vec_e.append((whole_invert, b))
                 elif phase == 3:
-                    vec_a.append((whole_floor, b))
-                    vec_b.append((whole_invert, b))
                     pe_mid.append((turn_back, b, 0))
                     act_last.append((store, b, 0))
                     pe_last.append((turn_back, b, 1))
@@ -397,21 +404,20 @@ def tile_wassvladlayer_pb_kernel(tc, probs, x, mu, sigma, out):
                 flip_x(0, 0, UNIT_PASSES // 2)
                 square_scalar(0)
                 flip_x(0, UNIT_PASSES // 2)
+                for bank in range(BANKS):
+                    flip_p(0, bank)
             else:
                 flip_x(step)
             if step + LOADS_AHEAD < UNITS:
                 load_x(step + LOADS_AHEAD)
             if step >= 1 and step % BATCH_UNITS == 1 and step // BATCH_UNITS + 2 < BATCHES:
                 load_probs(step // BATCH_UNITS + 2)
-            for u in {2: [], 3: [0, 1]}.get(step, [step - 2]):
+            for u in ([step - 2], [step - 2], [], [step - 3, step - 2])[step % BATCH_UNITS]:
                 if u >= 0:
                     multiply(u, "m1", "x_mx")
                     multiply(u, "m2", "sq_mx")
-            run(pe_mid)
             run(vec_a)
             run(act_mid)
-            if step > 0:
-                square_scalar(step)
             if vector_unit >= 0:
                 square_vector(vector_unit)
                 run(vec_b)
@@ -419,6 +425,11 @@ def tile_wassvladlayer_pb_kernel(tc, probs, x, mu, sigma, out):
                 run(vec_c)
                 quantise_squares(vector_unit)
             run(vec_d)
+            run(pe_mid)
+            run(act_late)
+            run(vec_e)
+            if step > 0:
+                square_scalar(step)
             run(pe_last)
             run(act_last)
 
@@ -429,34 +440,32 @@ def tile_wassvladlayer_pb_kernel(tc, probs, x, mu, sigma, out):
         turn_back(b - 1, 0)
         turn_back(b - 1, 1)
         square_vector(last)
-        whole_floor(b - 1)
         quantise_x(last)
-        whole_invert(b - 1)
         multiply(last, "m1", "x_mx")
-        mean_residual(b, first)
-        variance(b, first)
-        floor_variance(b, first)
-        square_m1(b, second)
+        store(b - 1, 0)
+        store(b - 1, 1)
         quantise_squares(last)
         multiply(last, "m2", "sq_mx")
+        square_m1(b, second)
+        variance(b, first)
+        mean_residual(b, first)
+        floor_variance(b, first)
         deviation(b, first)
+        variance(b, second)
         add_squares(b, 0, HALF_FEATURES, 0)
         mean_residual(b, second)
-        deviation_residual(b, first)
-        variance(b, second)
-        add_squares(b, FEATURES, FEATURES + HALF_FEATURES, 1)
         floor_variance(b, second)
-        add_squares(b, HALF_FEATURES, FEATURES, 2)
         deviation(b, second)
+        add_squares(b, HALF_FEATURES, FEATURES, 2)
+        deviation_residual(b, first)
         deviation_residual(b, second)
+        add_squares(b, FEATURES, FEATURES + HALF_FEATURES, 1)
         add_squares(b, FEATURES + HALF_FEATURES, 2 * FEATURES, 3)
-        store(b - 1, 0, on_vector=True)
         add_energies(b)
         cluster_norm(b)
         norm_floor(b)
         norm_left(b)
         norm_invert(b)
-        store(b - 1, 1)
         add_left(b)
         scale_columns(b, 0)
         turn_back(b, 0)

@@ -31,6 +31,7 @@ BANKS = UNIT_VALUES // 2 // 512
 LOADS_AHEAD = 4
 SCALAR_SQUARES = UNIT_VALUES * 3 // 8
 EARLY_UNITS = 4
+DIAGONAL_BATCHES = 2
 EARLY_SCALAR_SQUARES = UNIT_VALUES // 2
 LAST_SCALAR_SQUARES = UNIT_VALUES * 3 // 4
 
@@ -260,15 +261,20 @@ def tile_wassvladlayer_pb_kernel(tc, probs, x, mu, sigma, out):
 
         def add_squares(b, first, stop, column):
             unread = tail_tile("unread", b, 2 * FEATURES)[:, first:stop]
-            energy = tail_tile("energies", b, 4)[:, column : column + 1]
+            energy = tail_tile("energies", b, 4)[:, column : column + 1] if column < 3 else tail_tile("last_energy", b, 1)
             nc.scalar.activation(out=unread, in_=held["feat", b][:, first:stop], func=ACT.Square, accum_out=energy)
 
         def add_energies(b):
-            nc.vector.reduce_sum(out=tail_tile("energy", b, 1), in_=held["energies", b], axis=mybir.AxisListType.X)
+            nc.vector.reduce_sum(out=tail_tile("energy", b, 1), in_=held["energies", b][:, 0:3], axis=mybir.AxisListType.X)
 
         def cluster_norm(b):
-            energy = held["energy", b] if b == BATCHES - 1 else held["energies", b][:, 0:1]
-            nc.scalar.activation(out=tail_tile("norm", b, 1), in_=energy, func=ACT.Sqrt)
+            if b == BATCHES - 1:
+                rest = held["energy", b][:, 0:1]
+                nc.scalar.activation(
+                    out=tail_tile("norm", b, 1), in_=held["last_energy", b], func=ACT.Sqrt, bias=rest
+                )
+            else:
+                nc.scalar.activation(out=tail_tile("norm", b, 1), in_=held["energies", b][:, 0:1], func=ACT.Sqrt)
 
         def norm_left(b):
             nc.vector.tensor_scalar(
@@ -286,6 +292,9 @@ def tile_wassvladlayer_pb_kernel(tc, probs, x, mu, sigma, out):
             nc.vector.tensor_scalar_mul(
                 out=tail_tile("scaled", b, 2 * FEATURES)[:, cols], in0=held["feat", b][:, cols], scalar1=held["inverse", b][:, 0:1]
             )
+
+        def make_diagonal(b):
+            nc.vector.tensor_scalar_mul(out=tail_tile("diagonal", b, P), in0=ident, scalar1=held["inverse", b][:, 0:1])
 
         def add_left(b):
             held["whole", b] = flip_psum.tile([P, 1], F32, name="whole", tag="flipped")
@@ -305,17 +314,36 @@ def tile_wassvladlayer_pb_kernel(tc, probs, x, mu, sigma, out):
             held["back", b, h] = flip_psum.tile([P, CHUNKS, P], F32, name="back", tag="flipped")
             for c in range(CHUNKS):
                 first = h * FEATURES + c * P
-                nc.tensor.transpose(held["back", b, h][:, c, :], held["scaled", b][:, first : first + P], ident)
+                if b >= DIAGONAL_BATCHES:
+                    nc.tensor.transpose(held["back", b, h][:, c, :], held["scaled", b][:, first : first + P], ident)
+                else:
+                    nc.tensor.matmul(
+                        out=held["back", b, h][:, c, :],
+                        lhsT=held["feat", b][:, first : first + P],
+                        rhs=held["diagonal", b],
+                        start=True,
+                        stop=True,
+                    )
 
         def store(b, h, on_vector=False):
             rows = out[b].rearrange("(h p ck) -> h p ck", h=2, p=P)
             result = tail_pool.tile([P, FEATURES], F32, name="result_%d" % h)
             back = held["back", b, h].rearrange("p c k -> p (c k)")
-            if on_vector:
-                nc.vector.tensor_scalar_mul(out=result, in0=back, scalar1=held["whole_inverse", b][:, 0:1])
-            else:
-                nc.scalar.activation(out=result, in_=back, func=ACT.Copy, scale=held["whole_inverse", b][:, 0:1])
-            nc.sync.dma_start(out=rows[h], in_=result)
+            for cols in HALVES if b == BATCHES - 1 else (ALL,):
+                if on_vector:
+                    nc.vector.tensor_scalar_mul(
+                        out=result[:, cols], in0=back[:, cols], scalar1=held["whole_inverse", b][:, 0:1]
+                    )
+                else:
+                    nc.scalar.activation(
+                        out=result[:, cols], in_=back[:, cols], func=ACT.Copy, scale=held["whole_inverse", b][:, 0:1]
+                    )
+                nc.sync.dma_start(out=rows[h][:, cols], in_=result[:, cols])
+
+        def keep_warm(count, values):
+            unread = flip_psum.tile([P, 512], F32, name="unread_product", tag="flipped")
+            for i in range(count):
+                nc.tensor.matmul(out=unread, lhsT=values[:, :P], rhs=values, start=True, stop=True)
 
         def run(work):
             for stage, *args in work:
@@ -333,6 +361,9 @@ def tile_wassvladlayer_pb_kernel(tc, probs, x, mu, sigma, out):
         sigma_raw = load_param(sigma, "sigma")
         load_x(3)
 
+        filler = consts.tile([P, 512], BF16, name="filler")
+        nc.vector.memset(filler, 0.0)
+        keep_warm(5, filler)
         ident = consts.tile([P, P], F32, name="ident")
         make_identity(nc, ident)
         ident_bf16 = consts.tile([P, P], BF16, name="ident_bf16")
@@ -388,8 +419,11 @@ def tile_wassvladlayer_pb_kernel(tc, probs, x, mu, sigma, out):
                     vec_b.append((norm_floor, b))
                     vec_c.append((norm_invert, b))
                     pe_mid.append((add_left, b))
-                    vec_d.append((scale_columns, b, 0))
-                    vec_d.append((scale_columns, b, 1))
+                    if b < DIAGONAL_BATCHES:
+                        vec_d.append((make_diagonal, b))
+                    else:
+                        vec_d.append((scale_columns, b, 0))
+                        vec_d.append((scale_columns, b, 1))
                     act_late.append((whole_norm, b))
                     vec_e.append((whole_floor, b))
                     vec_e.append((whole_invert, b))
@@ -404,10 +438,11 @@ def tile_wassvladlayer_pb_kernel(tc, probs, x, mu, sigma, out):
                 flip_x(0, 0, UNIT_PASSES // 2)
                 square_scalar(0)
                 flip_x(0, UNIT_PASSES // 2)
-                for bank in range(BANKS):
-                    flip_p(0, bank)
             else:
                 flip_x(step)
+            if step == 1:
+                for bank in range(BANKS):
+                    flip_p(0, bank)
             if step + LOADS_AHEAD < UNITS:
                 load_x(step + LOADS_AHEAD)
             if step >= 1 and step % BATCH_UNITS == 1 and step // BATCH_UNITS + 2 < BATCHES:
@@ -439,6 +474,7 @@ def tile_wassvladlayer_pb_kernel(tc, probs, x, mu, sigma, out):
         multiply(last - 1, "m2", "sq_mx")
         turn_back(b - 1, 0)
         turn_back(b - 1, 1)
+        keep_warm(4, filler)
         square_vector(last)
         quantise_x(last)
         multiply(last, "m1", "x_mx")
@@ -446,6 +482,7 @@ def tile_wassvladlayer_pb_kernel(tc, probs, x, mu, sigma, out):
         store(b - 1, 1)
         quantise_squares(last)
         multiply(last, "m2", "sq_mx")
+        keep_warm(8, filler)
         square_m1(b, second)
         variance(b, first)
         mean_residual(b, first)
@@ -460,8 +497,8 @@ def tile_wassvladlayer_pb_kernel(tc, probs, x, mu, sigma, out):
         deviation_residual(b, first)
         deviation_residual(b, second)
         add_squares(b, FEATURES, FEATURES + HALF_FEATURES, 1)
-        add_squares(b, FEATURES + HALF_FEATURES, 2 * FEATURES, 3)
         add_energies(b)
+        add_squares(b, FEATURES + HALF_FEATURES, 2 * FEATURES, 3)
         cluster_norm(b)
         norm_floor(b)
         norm_left(b)

@@ -31,7 +31,8 @@ BANKS = UNIT_VALUES // 2 // 512
 LOADS_AHEAD = 4
 SCALAR_SQUARES = UNIT_VALUES * 3 // 8
 EARLY_UNITS = 4
-DIAGONAL_BATCHES = 2
+FIRST_SQUARES = 1024
+DIAGONAL_BATCHES = 0
 EARLY_SCALAR_SQUARES = UNIT_VALUES // 2
 LAST_SCALAR_SQUARES = UNIT_VALUES * 3 // 4
 
@@ -167,9 +168,10 @@ def tile_wassvladlayer_pb_kernel(tc, probs, x, mu, sigma, out):
                 return LAST_SCALAR_SQUARES
             return EARLY_SCALAR_SQUARES if u < EARLY_UNITS else SCALAR_SQUARES
 
-        def square_scalar(u):
-            held["squares", u] = grouped_pool.tile([P, UNIT_VALUES], BF16, name="sq_grouped", align_bytes=64)
-            part = slice(0, scalar_share(u))
+        def square_scalar(u, first=0, stop=None):
+            if first == 0:
+                held["squares", u] = grouped_pool.tile([P, UNIT_VALUES], BF16, name="sq_grouped", align_bytes=64)
+            part = slice(first, stop or scalar_share(u))
             nc.scalar.activation(out=held["squares", u][:, part], in_=held["x_grouped", u][:, part], func=ACT.Square)
 
         def square_vector(u):
@@ -183,6 +185,19 @@ def tile_wassvladlayer_pb_kernel(tc, probs, x, mu, sigma, out):
 
         def quantise_squares(u):
             held["sq_mx", u] = quantise(codes_pool, held["squares", u], "sq")
+
+        def quantise_squares_by_halves(u):
+            codes = codes_pool.tile([P, UNIT_VALUES // 4], U32, name="sq_codes", align_bytes=64)
+            scales = codes_pool.tile([P, UNIT_VALUES // 4], U8, name="sq_scales", align_bytes=64)
+            half = UNIT_VALUES // 2
+            for first in (0, half):
+                words = slice(first // 4, (first + half) // 4)
+                nc.vector.quantize_mx(
+                    out=codes[:, words].bitcast(FP8X4),
+                    scales=scales[:, words],
+                    in_=held["squares", u][:, first : first + half],
+                )
+            held["sq_mx", u] = (codes, scales)
 
         def acc_key(b, half_f):
             return (b, half_f if b == BATCHES - 1 else 0)
@@ -363,7 +378,6 @@ def tile_wassvladlayer_pb_kernel(tc, probs, x, mu, sigma, out):
 
         filler = consts.tile([P, 512], BF16, name="filler")
         nc.vector.memset(filler, 0.0)
-        keep_warm(5, filler)
         ident = consts.tile([P, P], F32, name="ident")
         make_identity(nc, ident)
         ident_bf16 = consts.tile([P, P], BF16, name="ident_bf16")
@@ -436,8 +450,9 @@ def tile_wassvladlayer_pb_kernel(tc, probs, x, mu, sigma, out):
             run(act_first)
             if step == 0:
                 flip_x(0, 0, UNIT_PASSES // 2)
-                square_scalar(0)
+                square_scalar(0, 0, FIRST_SQUARES)
                 flip_x(0, UNIT_PASSES // 2)
+                square_scalar(0, FIRST_SQUARES)
             else:
                 flip_x(step)
             if step == 1:
@@ -473,26 +488,25 @@ def tile_wassvladlayer_pb_kernel(tc, probs, x, mu, sigma, out):
         multiply(last - 1, "m1", "x_mx")
         multiply(last - 1, "m2", "sq_mx")
         turn_back(b - 1, 0)
-        turn_back(b - 1, 1)
-        keep_warm(4, filler)
+        keep_warm(5, filler)
         square_vector(last)
         quantise_x(last)
         multiply(last, "m1", "x_mx")
         store(b - 1, 0)
-        store(b - 1, 1)
-        quantise_squares(last)
+        quantise_squares_by_halves(last)
         multiply(last, "m2", "sq_mx")
+        turn_back(b - 1, 1)
         keep_warm(8, filler)
         square_m1(b, second)
-        variance(b, first)
         mean_residual(b, first)
+        variance(b, first)
+        add_squares(b, 0, HALF_FEATURES, 0)
+        variance(b, second)
         floor_variance(b, first)
         deviation(b, first)
-        variance(b, second)
-        add_squares(b, 0, HALF_FEATURES, 0)
-        mean_residual(b, second)
         floor_variance(b, second)
         deviation(b, second)
+        mean_residual(b, second)
         add_squares(b, HALF_FEATURES, FEATURES, 2)
         deviation_residual(b, first)
         deviation_residual(b, second)
@@ -503,13 +517,14 @@ def tile_wassvladlayer_pb_kernel(tc, probs, x, mu, sigma, out):
         norm_floor(b)
         norm_left(b)
         norm_invert(b)
+        store(b - 1, 1)
         add_left(b)
         scale_columns(b, 0)
         turn_back(b, 0)
-        scale_columns(b, 1)
-        turn_back(b, 1)
         whole_norm(b)
         whole_floor(b)
+        scale_columns(b, 1)
+        turn_back(b, 1)
         whole_invert(b)
         store(b, 0)
         store(b, 1, on_vector=True)

@@ -95,8 +95,16 @@ def tile_wassvladlayer_pb_kernel(tc, probs, x, mu, sigma, out):
             nc.scalar.copy(out=rows, in_=back.rearrange("p c d -> p (c d)"))
             held[name] = rows
 
-        def flip_bank(blocks, grouped_words, copy):
+        def flip_bank(blocks, grouped_words, copy, warm=False):
             flipped = flip_psum.tile([P, BLOCKS_A_BANK, 2, P], F32, name="flipped")
+            if warm:
+                nc.tensor.matmul(
+                    out=flipped.rearrange("q i half row -> q (i half row)"),
+                    lhsT=filler[:, :P],
+                    rhs=filler,
+                    start=True,
+                    stop=True,
+                )
             for i, words in enumerate(blocks):
                 for half in range(2):
                     nc.tensor.transpose(flipped[:, i, half, :], words[:, half * P : (half + 1) * P], ident)
@@ -159,6 +167,7 @@ def tile_wassvladlayer_pb_kernel(tc, probs, x, mu, sigma, out):
                     held["x_words", u, g],
                     word_blocks(held["x_grouped", u])[:, g * UNIT_CHUNKS : (g + 1) * UNIT_CHUNKS],
                     nc.scalar.copy,
+                    g in (0,) and u > 0,
                 )
 
         def scalar_share(u):
@@ -419,7 +428,6 @@ def tile_wassvladlayer_pb_kernel(tc, probs, x, mu, sigma, out):
             for b in range(BATCHES - 1):
                 phase = step - BATCH_UNITS * (b + 1) - 1
                 if phase == 0:
-                    act_mid.append((square_m1, b, ALL))
                     vec_c.append((mean_residual, b, ALL))
                     vec_d.append((variance, b, ALL))
                 elif phase == 1:
@@ -453,6 +461,12 @@ def tile_wassvladlayer_pb_kernel(tc, probs, x, mu, sigma, out):
                 square_scalar(0, 0, FIRST_SQUARES)
                 flip_x(0, UNIT_PASSES // 2)
                 square_scalar(0, FIRST_SQUARES)
+            elif step > BATCH_UNITS and step % BATCH_UNITS == 1:
+                flip_x(step, 0, UNIT_PASSES // 2)
+                multiply(step - 2, "m1", "x_mx")
+                multiply(step - 2, "m2", "sq_mx")
+                square_m1(step // BATCH_UNITS - 1, ALL)
+                flip_x(step, UNIT_PASSES // 2)
             else:
                 flip_x(step)
             if step == 1:
@@ -462,7 +476,7 @@ def tile_wassvladlayer_pb_kernel(tc, probs, x, mu, sigma, out):
                 load_x(step + LOADS_AHEAD)
             if step >= 1 and step % BATCH_UNITS == 1 and step // BATCH_UNITS + 2 < BATCHES:
                 load_probs(step // BATCH_UNITS + 2)
-            for u in ([step - 2], [step - 2], [], [step - 3, step - 2])[step % BATCH_UNITS]:
+            for u in ([step - 2], [], [], [step - 3, step - 2])[step % BATCH_UNITS]:
                 if u >= 0:
                     multiply(u, "m1", "x_mx")
                     multiply(u, "m2", "sq_mx")
@@ -488,7 +502,6 @@ def tile_wassvladlayer_pb_kernel(tc, probs, x, mu, sigma, out):
         multiply(last - 1, "m1", "x_mx")
         multiply(last - 1, "m2", "sq_mx")
         turn_back(b - 1, 0)
-        keep_warm(5, filler)
         square_vector(last)
         quantise_x(last)
         multiply(last, "m1", "x_mx")

@@ -29,12 +29,12 @@ UNITS = BATCHES * BATCH_UNITS
 BLOCKS_A_BANK = 2
 BANKS = UNIT_VALUES // 2 // 512
 LOADS_AHEAD = 4
-SCALAR_SQUARES = UNIT_VALUES * 3 // 8
+SCALAR_SQUARES = UNIT_VALUES * 5 // 16
 EARLY_UNITS = 4
 FIRST_SQUARES = 1024
-DIAGONAL_BATCHES = 0
+DIAGONAL_BATCHES = 3
 EARLY_SCALAR_SQUARES = UNIT_VALUES // 2
-LAST_SCALAR_SQUARES = UNIT_VALUES * 3 // 4
+LAST_SCALAR_SQUARES = UNIT_VALUES * 5 // 8
 
 
 def tile_wassvladlayer_pb_kernel(tc, probs, x, mu, sigma, out):
@@ -95,9 +95,9 @@ def tile_wassvladlayer_pb_kernel(tc, probs, x, mu, sigma, out):
             nc.scalar.copy(out=rows, in_=back.rearrange("p c d -> p (c d)"))
             held[name] = rows
 
-        def flip_bank(blocks, grouped_words, copy, warm=False):
+        def flip_bank(blocks, grouped_words, copy, warm=0):
             flipped = flip_psum.tile([P, BLOCKS_A_BANK, 2, P], F32, name="flipped")
-            if warm:
+            for i in range(warm):
                 nc.tensor.matmul(
                     out=flipped.rearrange("q i half row -> q (i half row)"),
                     lhsT=filler[:, :P],
@@ -167,7 +167,7 @@ def tile_wassvladlayer_pb_kernel(tc, probs, x, mu, sigma, out):
                     held["x_words", u, g],
                     word_blocks(held["x_grouped", u])[:, g * UNIT_CHUNKS : (g + 1) * UNIT_CHUNKS],
                     nc.scalar.copy,
-                    g in (0,) and u > 0,
+                    (3 if u == 1 else 0) if g == 0 and u > 0 else 0,
                 )
 
         def scalar_share(u):
@@ -414,7 +414,7 @@ def tile_wassvladlayer_pb_kernel(tc, probs, x, mu, sigma, out):
                     vec_c.append((sum_p, b, 1))
                     vec_d.append((invert_p, b))
                 if step == begin + 2:
-                    vec_a.append((scale_p, b))
+                    vec_b.append((scale_p, b))
                 for bank in range(BANKS):
                     if step == max(BATCH_UNITS * b - 3 + bank, begin + 2 + bank // 2):
                         pe_last.append((flip_p, b, bank))
@@ -428,8 +428,8 @@ def tile_wassvladlayer_pb_kernel(tc, probs, x, mu, sigma, out):
             for b in range(BATCHES - 1):
                 phase = step - BATCH_UNITS * (b + 1) - 1
                 if phase == 0:
-                    vec_c.append((mean_residual, b, ALL))
-                    vec_d.append((variance, b, ALL))
+                    vec_c.append((variance, b, ALL))
+                    vec_d.append((mean_residual, b, ALL))
                 elif phase == 1:
                     vec_a.append((floor_variance, b, ALL))
                     act_mid.append((deviation, b, ALL))
@@ -448,8 +448,8 @@ def tile_wassvladlayer_pb_kernel(tc, probs, x, mu, sigma, out):
                         vec_d.append((scale_columns, b, 1))
                     act_late.append((whole_norm, b))
                     vec_e.append((whole_floor, b))
-                    vec_e.append((whole_invert, b))
                 elif phase == 3:
+                    vec_b.append((whole_invert, b))
                     pe_mid.append((turn_back, b, 0))
                     act_last.append((store, b, 0))
                     pe_last.append((turn_back, b, 1))
@@ -503,13 +503,14 @@ def tile_wassvladlayer_pb_kernel(tc, probs, x, mu, sigma, out):
         multiply(last - 1, "m2", "sq_mx")
         turn_back(b - 1, 0)
         square_vector(last)
+        whole_invert(b - 1)
         quantise_x(last)
         multiply(last, "m1", "x_mx")
         store(b - 1, 0)
         quantise_squares_by_halves(last)
         multiply(last, "m2", "sq_mx")
         turn_back(b - 1, 1)
-        keep_warm(8, filler)
+        keep_warm(5, filler)
         square_m1(b, second)
         mean_residual(b, first)
         variance(b, first)

from contextlib import ExitStack

import concourse.mybir as mybir
from concourse.masks import make_identity

F32 = mybir.dt.float32
BF16 = mybir.dt.bfloat16
U32 = mybir.dt.uint32
U8 = mybir.dt.uint8
FP8X4 = mybir.dt.float8_e4m3fn_x4
ACT = mybir.ActivationFunctionType
ALU = mybir.AluOpType

P = 128
BATCHES, FEATURES, POINTS, CLUSTERS = 4, 512, 4096, 128
EPS = 1e-6
FLOPS = 2 * 2 * BATCHES * FEATURES * POINTS * CLUSTERS

PASS_POINTS = 4 * P
PASS_WORDS = PASS_POINTS // 2
PASSES = POINTS // PASS_POINTS
CHUNKS = FEATURES // P
HALF_POINTS = POINTS // 2
HALF_FEATURES = FEATURES // 2
UNIT_CHUNKS, UNIT_PASSES = CHUNKS // 2, PASSES // 2
UNIT_VALUES = UNIT_CHUNKS * HALF_POINTS
BATCH_UNITS = 4
UNITS = BATCHES * BATCH_UNITS
BLOCKS_A_BANK = 2
BANKS = UNIT_VALUES // 2 // 512
LOADS_AHEAD = 4
SCALAR_SQUARES = UNIT_VALUES * 5 // 16
EARLY_UNITS = 4
FIRST_SQUARES = 1024
DIAGONAL_BATCHES = 3
EARLY_SCALAR_SQUARES = UNIT_VALUES // 2
LAST_SCALAR_SQUARES = UNIT_VALUES * 5 // 8


def tile_wassvladlayer_pb_kernel(tc, probs, x, mu, sigma, out):
    nc = tc.nc
    with ExitStack() as pools:
        consts = pools.enter_context(tc.tile_pool(name="consts", bufs=1))
        x_pool = pools.enter_context(tc.tile_pool(name="x_pool", bufs=LOADS_AHEAD))
        p_raw_pool = pools.enter_context(tc.tile_pool(name="p_raw_pool", bufs=2))
        p_pool = pools.enter_context(tc.tile_pool(name="p_pool", bufs=2))
        p_codes_pool = pools.enter_context(tc.tile_pool(name="p_codes_pool", bufs=2))
        grouped_pool = pools.enter_context(tc.tile_pool(name="grouped_pool", bufs=3))
        codes_pool = pools.enter_context(tc.tile_pool(name="codes_pool", bufs=4))
        tail_pool = pools.enter_context(tc.tile_pool(name="tail_pool", bufs=2))
        flip_psum = pools.enter_context(tc.psum_pool(name="flip_psum", bufs=6))
        acc_psum = pools.enter_context(tc.psum_pool(name="acc_psum", bufs=1))
        pools.enter_context(tc.manual_schedule())

        held = {}

        def load_probs_half(b, half):
            if half == 0:
                held["p_raw", b] = p_raw_pool.tile([P, POINTS], BF16, name="p_raw")
            cols = slice(half * HALF_POINTS, (half + 1) * HALF_POINTS)
            nc.sync.dma_start(out=held["p_raw", b][:, cols], in_=probs[b][:, cols])

        def load_probs(b):
            for half in range(2):
                load_probs_half(b, half)

        def load_x(u, first=0, points=HALF_POINTS):
            b, part = divmod(u, BATCH_UNITS)
            half_f, half_n = divmod(part, 2)
            if first == 0:
                held["x_raw", u] = x_pool.tile([P, UNIT_VALUES], BF16, name="x_raw")
            rows = x[b].rearrange("(p c) n -> p c n", c=CHUNKS)
            start = half_n * HALF_POINTS + first
            piece = held["x_raw", u][:, UNIT_CHUNKS * first : UNIT_CHUNKS * (first + points)]
            piece = piece.rearrange("p (c n) -> p c n", c=UNIT_CHUNKS)
            words = piece.bitcast(F32)
            for g in range(points // PASS_POINTS):
                cols = slice(g * PASS_WORDS, (g + 1) * PASS_WORDS)
                held["x_words", u, first // PASS_POINTS + g] = [words[:, c, cols] for c in range(UNIT_CHUNKS)]
            nc.sync.dma_start(
                out=piece,
                in_=rows[:, half_f * UNIT_CHUNKS : (half_f + 1) * UNIT_CHUNKS, start : start + points],
            )

        def load_param(param, name):
            raw = consts.tile([P, CHUNKS, CLUSTERS], BF16, name=name + "_raw")
            nc.sync.dma_start(out=raw, in_=param[0].rearrange("(p c) k -> p c k", c=CHUNKS))
            return raw

        def cluster_rows(raw, name):
            back = flip_psum.tile([P, CHUNKS, P], BF16, name="param_back", tag="flipped")
            for c in range(CHUNKS):
                nc.tensor.transpose(back[:, c, :], raw[:, c, :], ident_bf16)
            rows = consts.tile([P, FEATURES], BF16, name=name + "_rows")
            nc.scalar.copy(out=rows, in_=back.rearrange("p c d -> p (c d)"))
            held[name] = rows

        def flip_bank(blocks, grouped_words, copy, warm=0):
            flipped = flip_psum.tile([P, BLOCKS_A_BANK, 2, P], F32, name="flipped")
            for i in range(warm):
                nc.tensor.matmul(
                    out=flipped.rearrange("q i half row -> q (i half row)"),
                    lhsT=filler[:, :P],
                    rhs=filler,
                    start=True,
                    stop=True,
                )
            for i, words in enumerate(blocks):
                for half in range(2):
                    nc.tensor.transpose(flipped[:, i, half, :], words[:, half * P : (half + 1) * P], ident)
            copy(out=grouped_words, in_=flipped.rearrange("q i half row -> q i row half"))

        def word_blocks(grouped):
            return grouped.bitcast(F32).rearrange("q (blk row half) -> q blk row half", row=P, half=2)

        def quantise(pool, grouped, name):
            codes = pool.tile([P, UNIT_VALUES // 4], U32, name=name + "_codes", align_bytes=64)
            scales = pool.tile([P, UNIT_VALUES // 4], U8, name=name + "_scales", align_bytes=64)
            nc.vector.quantize_mx(out=codes.bitcast(FP8X4), scales=scales, in_=grouped)
            return codes, scales

        def sum_p(b, half):
            if half == 0:
                held["p_rows", b] = p_pool.tile([P, POINTS], BF16, name="p_rows")
            cols = slice(half * HALF_POINTS, (half + 1) * HALF_POINTS)
            so_far = held["p_total", b] if half else EPS
            total = p_pool.tile([P, 1], F32, name="p_total_%d" % half)
            nc.vector.tensor_scalar(
                out=held["p_rows", b][:, cols],
                in0=held["p_raw", b][:, cols],
                scalar1=1.0,
                scalar2=so_far,
                op0=ALU.mult,
                op1=ALU.add,
                accum_out=total,
            )
            held["p_total", b] = total

        def invert_p(b):
            held["p_share", b] = p_pool.tile([P, 1], F32, name="p_share")
            nc.vector.reciprocal(out=held["p_share", b], in_=held["p_total", b])

        def scale_p(b):
            nc.vector.tensor_scalar_mul(
                out=held["p_rows", b], in0=held["p_raw", b], scalar1=held["p_share", b][:, 0:1]
            )

        def flip_p(b, bank):
            if bank == 0:
                held["p_grouped", b] = p_pool.tile([P, POINTS], BF16, name="p_grouped", align_bytes=64)
            words = held["p_rows", b].bitcast(F32)
            passes = range(bank * BLOCKS_A_BANK, (bank + 1) * BLOCKS_A_BANK)
            flip_bank(
                [words[:, g * PASS_WORDS : (g + 1) * PASS_WORDS] for g in passes],
                word_blocks(held["p_grouped", b])[:, bank * BLOCKS_A_BANK : (bank + 1) * BLOCKS_A_BANK],
                nc.scalar.copy,
            )

        def quantise_p(b):
            held["p_mx", b] = quantise(p_codes_pool, held["p_grouped", b], "p")

        def flip_x(u, first=0, stop=UNIT_PASSES):
            if first == 0:
                held["x_grouped", u] = grouped_pool.tile([P, UNIT_VALUES], BF16, name="x_grouped", align_bytes=64)
            for g in range(first, stop):
                flip_bank(
                    held["x_words", u, g],
                    word_blocks(held["x_grouped", u])[:, g * UNIT_CHUNKS : (g + 1) * UNIT_CHUNKS],
                    nc.scalar.copy,
                    (3 if u == 1 else 0) if g == 0 and u > 0 else 0,
                )

        def scalar_share(u):
            if u == 0:
                return UNIT_VALUES // 2
            if u == UNITS - 1:
                return LAST_SCALAR_SQUARES
            return EARLY_SCALAR_SQUARES if u < EARLY_UNITS else SCALAR_SQUARES

        def square_scalar(u, first=0, stop=None):
            if first == 0:
                held["squares", u] = grouped_pool.tile([P, UNIT_VALUES], BF16, name="sq_grouped", align_bytes=64)
            part = slice(first, stop or scalar_share(u))
            nc.scalar.activation(out=held["squares", u][:, part], in_=held["x_grouped", u][:, part], func=ACT.Square)

        def square_vector(u):
            part = slice(scalar_share(u), UNIT_VALUES)
            if part.start < part.stop:
                values = held["x_grouped", u][:, part]
                nc.vector.tensor_tensor(out=held["squares", u][:, part], in0=values, in1=values, op=ALU.mult)

        def quantise_x(u):
            held["x_mx", u] = quantise(codes_pool, held["x_grouped", u], "x")

        def quantise_squares(u):
            held["sq_mx", u] = quantise(codes_pool, held["squares", u], "sq")

        def quantise_squares_by_halves(u):
            codes = codes_pool.tile([P, UNIT_VALUES // 4], U32, name="sq_codes", align_bytes=64)
            scales = codes_pool.tile([P, UNIT_VALUES // 4], U8, name="sq_scales", align_bytes=64)
            half = UNIT_VALUES // 2
            for first in (0, half):
                words = slice(first // 4, (first + half) // 4)
                nc.vector.quantize_mx(
                    out=codes[:, words].bitcast(FP8X4),
                    scales=scales[:, words],
                    in_=held["squares", u][:, first : first + half],
                )
            held["sq_mx", u] = (codes, scales)

        def acc_key(b, half_f):
            return (b, half_f if b == BATCHES - 1 else 0)

        def multiply(u, moment, operand):
            b, part = divmod(u, BATCH_UNITS)
            half_f, half_n = divmod(part, 2)
            key = (moment, acc_key(b, half_f))
            if key not in held:
                if u < UNITS - 2:
                    held[key] = acc_psum.tile([P, FEATURES], F32, name=moment)
                else:
                    held[key] = flip_psum.tile([P, FEATURES], F32, name="last_" + moment, tag="flipped")
            acc = held[key][:, half_f * HALF_FEATURES : (half_f + 1) * HALF_FEATURES]
            p_codes, p_scales = held["p_mx", b]
            codes, scales = held[operand, u]
            for g in range(UNIT_PASSES):
                whole = half_n * UNIT_PASSES + g
                p_cols = slice(whole * CLUSTERS, (whole + 1) * CLUSTERS)
                x_cols = slice(g * HALF_FEATURES, (g + 1) * HALF_FEATURES)
                nc.tensor.matmul_mx(
                    out=acc,
                    lhsT=p_codes[:, p_cols].bitcast(FP8X4),
                    lhsT_scale=p_scales[:, p_cols],
                    rhs=codes[:, x_cols].bitcast(FP8X4),
                    rhs_scale=scales[:, x_cols],
                    start=(whole == 0),
                    stop=(whole == PASSES - 1),
                )

        ALL = slice(0, FEATURES)
        HALVES = (slice(0, HALF_FEATURES), slice(HALF_FEATURES, FEATURES))

        def moment_tile(moment, b, cols):
            return held[moment, acc_key(b, 0 if cols.start == 0 else 1)][:, cols]

        def tail_tile(what, b, width):
            if (what, b) not in held:
                held[what, b] = tail_pool.tile([P, width], F32, name=what)
            return held[what, b]

        def feat_tile(b, h, cols):
            return tail_tile("feat", b, 2 * FEATURES)[:, h * FEATURES + cols.start : h * FEATURES + cols.stop]

        def square_m1(b, cols):
            nc.scalar.activation(
                out=tail_tile("m1_squared", b, FEATURES)[:, cols], in_=moment_tile("m1", b, cols), func=ACT.Square
            )

        def mean_residual(b, cols):
            nc.vector.tensor_tensor(
                out=feat_tile(b, 0, cols), in0=moment_tile("m1", b, cols), in1=held["mu"][:, cols], op=ALU.subtract
            )

        def variance(b, cols):
            nc.vector.tensor_tensor(
                out=tail_tile("spread", b, FEATURES)[:, cols],
                in0=moment_tile("m2", b, cols),
                in1=held["m1_squared", b][:, cols],
                op=ALU.subtract,
            )

        def floor_variance(b, cols):
            spread = held["spread", b][:, cols]
            nc.vector.tensor_scalar_max(out=spread, in0=spread, scalar1=EPS)

        def deviation(b, cols):
            nc.scalar.activation(
                out=tail_tile("deviation", b, FEATURES)[:, cols], in_=held["spread", b][:, cols], func=ACT.Sqrt
            )

        def deviation_residual(b, cols):
            nc.vector.tensor_tensor(
                out=feat_tile(b, 1, cols), in0=held["deviation", b][:, cols], in1=held["sigma"][:, cols], op=ALU.subtract
            )

        def add_squares(b, first, stop, column):
            unread = tail_tile("unread", b, 2 * FEATURES)[:, first:stop]
            energy = tail_tile("energies", b, 4)[:, column : column + 1] if column < 3 else tail_tile("last_energy", b, 1)
            nc.scalar.activation(out=unread, in_=held["feat", b][:, first:stop], func=ACT.Square, accum_out=energy)

        def add_energies(b):
            nc.vector.reduce_sum(out=tail_tile("energy", b, 1), in_=held["energies", b][:, 0:3], axis=mybir.AxisListType.X)

        def cluster_norm(b):
            if b == BATCHES - 1:
                rest = held["energy", b][:, 0:1]
                nc.scalar.activation(
                    out=tail_tile("norm", b, 1), in_=held["last_energy", b], func=ACT.Sqrt, bias=rest
                )
            else:
                nc.scalar.activation(out=tail_tile("norm", b, 1), in_=held["energies", b][:, 0:1], func=ACT.Sqrt)

        def norm_left(b):
            nc.vector.tensor_scalar(
                out=tail_tile("left", b, 1), in0=held["norm", b], scalar1=1.0 / EPS, scalar2=1.0, op0=ALU.mult, op1=ALU.min
            )

        def norm_floor(b):
            nc.vector.tensor_scalar_max(out=tail_tile("floored", b, 1), in0=held["norm", b], scalar1=EPS)

        def norm_invert(b):
            nc.vector.reciprocal(out=tail_tile("inverse", b, 1), in_=held["floored", b])

        def scale_columns(b, h):
            cols = slice(h * FEATURES, (h + 1) * FEATURES)
            nc.vector.tensor_scalar_mul(
                out=tail_tile("scaled", b, 2 * FEATURES)[:, cols], in0=held["feat", b][:, cols], scalar1=held["inverse", b][:, 0:1]
            )

        def make_diagonal(b):
            nc.vector.tensor_scalar_mul(out=tail_tile("diagonal", b, P), in0=ident, scalar1=held["inverse", b][:, 0:1])

        def add_left(b):
            held["whole", b] = flip_psum.tile([P, 1], F32, name="whole", tag="flipped")
            left = held["left", b]
            nc.tensor.matmul(out=held["whole", b], lhsT=left[:, 0:1].to_broadcast([P, P]), rhs=left, start=True, stop=True)

        def whole_norm(b):
            nc.scalar.activation(out=tail_tile("whole_norm", b, 1), in_=held["whole", b], func=ACT.Sqrt)

        def whole_floor(b):
            nc.vector.tensor_scalar_max(out=tail_tile("whole_floored", b, 1), in0=held["whole_norm", b], scalar1=EPS)

        def whole_invert(b):
            nc.vector.reciprocal(out=tail_tile("whole_inverse", b, 1), in_=held["whole_floored", b])

        def turn_back(b, h):
            held["back", b, h] = flip_psum.tile([P, CHUNKS, P], F32, name="back", tag="flipped")
            for c in range(CHUNKS):
                first = h * FEATURES + c * P
                if b >= DIAGONAL_BATCHES:
                    nc.tensor.transpose(held["back", b, h][:, c, :], held["scaled", b][:, first : first + P], ident)
                else:
                    nc.tensor.matmul(
                        out=held["back", b, h][:, c, :],
                        lhsT=held["feat", b][:, first : first + P],
                        rhs=held["diagonal", b],
                        start=True,
                        stop=True,
                    )

        def store(b, h, on_vector=False):
            rows = out[b].rearrange("(h p ck) -> h p ck", h=2, p=P)
            result = tail_pool.tile([P, FEATURES], F32, name="result_%d" % h)
            back = held["back", b, h].rearrange("p c k -> p (c k)")
            for cols in HALVES if b == BATCHES - 1 else (ALL,):
                if on_vector:
                    nc.vector.tensor_scalar_mul(
                        out=result[:, cols], in0=back[:, cols], scalar1=held["whole_inverse", b][:, 0:1]
                    )
                else:
                    nc.scalar.activation(
                        out=result[:, cols], in_=back[:, cols], func=ACT.Copy, scale=held["whole_inverse", b][:, 0:1]
                    )
                nc.sync.dma_start(out=rows[h][:, cols], in_=result[:, cols])

        def keep_warm(count, values):
            unread = flip_psum.tile([P, 512], F32, name="unread_product", tag="flipped")
            for i in range(count):
                nc.tensor.matmul(out=unread, lhsT=values[:, :P], rhs=values, start=True, stop=True)

        def run(work):
            for stage, *args in work:
                stage(*args)

        load_x(0, 0, PASS_POINTS)
        load_probs_half(0, 0)
        load_x(0, PASS_POINTS, PASS_POINTS)
        load_probs_half(0, 1)
        load_x(0, 2 * PASS_POINTS, 2 * PASS_POINTS)
        load_x(1)
        load_probs(1)
        load_x(2)
        mu_raw = load_param(mu, "mu")
        sigma_raw = load_param(sigma, "sigma")
        load_x(3)

        filler = consts.tile([P, 512], BF16, name="filler")
        nc.vector.memset(filler, 0.0)
        ident = consts.tile([P, P], F32, name="ident")
        make_identity(nc, ident)
        ident_bf16 = consts.tile([P, P], BF16, name="ident_bf16")
        make_identity(nc, ident_bf16)
        one = consts.tile([P, 1], F32, name="one")
        nc.vector.memset(one, 1.0)
        root_of_one = consts.tile([P, 1], F32, name="root_of_one")
        nc.scalar.activation(out=root_of_one, in_=one, func=ACT.Sqrt)

        sum_p(0, 0)
        sum_p(0, 1)
        invert_p(0)
        scale_p(0)
        for step in range(UNITS):
            vector_unit = step - 1
            vec_a, vec_b, vec_c, vec_d, vec_e = [], [], [], [], []
            act_first, act_mid, act_late, act_last, pe_mid, pe_last = [], [], [], [], [], []
            if step == UNITS - 1:
                act_mid.append((square_m1, BATCHES - 1, HALVES[0]))
            for b in range(1, BATCHES):
                begin = max(BATCH_UNITS * (b - 1) - 1, 1)
                if step == begin:
                    vec_c.append((sum_p, b, 0))
                if step == begin + 1:
                    vec_c.append((sum_p, b, 1))
                    vec_d.append((invert_p, b))
                if step == begin + 2:
                    vec_b.append((scale_p, b))
                for bank in range(BANKS):
                    if step == max(BATCH_UNITS * b - 3 + bank, begin + 2 + bank // 2):
                        pe_last.append((flip_p, b, bank))
                if step == BATCH_UNITS * b + 1:
                    vec_c.append((quantise_p, b))
            if step == 2:
                vec_b.append((quantise_p, 0))
            if step == 3:
                pe_last.append((cluster_rows, mu_raw, "mu"))
                pe_last.append((cluster_rows, sigma_raw, "sigma"))
            for b in range(BATCHES - 1):
                phase = step - BATCH_UNITS * (b + 1) - 1
                if phase == 0:
                    vec_c.append((variance, b, ALL))
                    vec_d.append((mean_residual, b, ALL))
                elif phase == 1:
                    vec_a.append((floor_variance, b, ALL))
                    act_mid.append((deviation, b, ALL))
                    vec_c.append((deviation_residual, b, ALL))
                    act_last.append((add_squares, b, 0, 2 * FEATURES, 0))
                elif phase == 2:
                    act_first.append((cluster_norm, b))
                    vec_b.append((norm_left, b))
                    vec_b.append((norm_floor, b))
                    vec_c.append((norm_invert, b))
                    pe_mid.append((add_left, b))
                    if b < DIAGONAL_BATCHES:
                        vec_d.append((make_diagonal, b))
                    else:
                        vec_d.append((scale_columns, b, 0))
                        vec_d.append((scale_columns, b, 1))
                    act_late.append((whole_norm, b))
                    vec_e.append((whole_floor, b))
                elif phase == 3:
                    vec_b.append((whole_invert, b))
                    pe_mid.append((turn_back, b, 0))
                    act_last.append((store, b, 0))
                    pe_last.append((turn_back, b, 1))
                    act_last.append((store, b, 1))

            run(act_first)
            if step == 0:
                flip_x(0, 0, UNIT_PASSES // 2)
                square_scalar(0, 0, FIRST_SQUARES)
                flip_x(0, UNIT_PASSES // 2)
                square_scalar(0, FIRST_SQUARES)
            elif step > BATCH_UNITS and step % BATCH_UNITS == 1:
                flip_x(step, 0, UNIT_PASSES // 2)
                multiply(step - 2, "m1", "x_mx")
                multiply(step - 2, "m2", "sq_mx")
                square_m1(step // BATCH_UNITS - 1, ALL)
                flip_x(step, UNIT_PASSES // 2)
            else:
                flip_x(step)
            if step == 1:
                for bank in range(BANKS):
                    flip_p(0, bank)
            if step + LOADS_AHEAD < UNITS:
                load_x(step + LOADS_AHEAD)
            if step >= 1 and step % BATCH_UNITS == 1 and step // BATCH_UNITS + 2 < BATCHES:
                load_probs(step // BATCH_UNITS + 2)
            for u in ([step - 2], [], [], [step - 3, step - 2])[step % BATCH_UNITS]:
                if u >= 0:
                    multiply(u, "m1", "x_mx")
                    multiply(u, "m2", "sq_mx")
            run(vec_a)
            run(act_mid)
            if vector_unit >= 0:
                square_vector(vector_unit)
                run(vec_b)
                quantise_x(vector_unit)
                run(vec_c)
                quantise_squares(vector_unit)
            run(vec_d)
            run(pe_mid)
            run(act_late)
            run(vec_e)
            if step > 0:
                square_scalar(step)
            run(pe_last)
            run(act_last)

        b, last = BATCHES - 1, UNITS - 1
        first, second = HALVES
        multiply(last - 1, "m1", "x_mx")
        multiply(last - 1, "m2", "sq_mx")
        turn_back(b - 1, 0)
        square_vector(last)
        whole_invert(b - 1)
        quantise_x(last)
        multiply(last, "m1", "x_mx")
        store(b - 1, 0)
        quantise_squares_by_halves(last)
        multiply(last, "m2", "sq_mx")
        turn_back(b - 1, 1)
        keep_warm(5, filler)
        square_m1(b, second)
        mean_residual(b, first)
        variance(b, first)
        add_squares(b, 0, HALF_FEATURES, 0)
        variance(b, second)
        floor_variance(b, first)
        deviation(b, first)
        floor_variance(b, second)
        deviation(b, second)
        mean_residual(b, second)
        add_squares(b, HALF_FEATURES, FEATURES, 2)
        deviation_residual(b, first)
        deviation_residual(b, second)
        add_squares(b, FEATURES, FEATURES + HALF_FEATURES, 1)
        add_energies(b)
        add_squares(b, FEATURES + HALF_FEATURES, 2 * FEATURES, 3)
        cluster_norm(b)
        norm_floor(b)
        norm_left(b)
        norm_invert(b)
        store(b - 1, 1)
        add_left(b)
        scale_columns(b, 0)
        turn_back(b, 0)
        whole_norm(b)
        whole_floor(b)
        scale_columns(b, 1)
        turn_back(b, 1)
        whole_invert(b)
        store(b, 0)
        store(b, 1, on_vector=True)
